import numpy as np
import ml_dtypes


def mxq(x, axis, fmt="e4m3"):
    dtype, down = {"e4m3": (ml_dtypes.float8_e4m3fn, 7), "e5m2": (ml_dtypes.float8_e5m2, 14)}[fmt]
    v = np.moveaxis(np.asarray(x, np.float32).astype(ml_dtypes.bfloat16).astype(np.float64), axis, -1)
    blocks = v.reshape(v.shape[:-1] + (-1, 32))
    amax = np.abs(blocks).max(-1, keepdims=True)
    byte = np.maximum(np.where(amax > 0, np.frexp(amax)[1] - 1 + 127, 0) - down, 1)
    scale = np.exp2(byte - 127.0)
    codes = (blocks / scale).astype(np.float32).astype(dtype).astype(np.float64)
    return np.moveaxis((codes * scale).reshape(v.shape), -1, axis)


WIDE = False


def mx_kscale(k):
    if not WIDE:
        return np.ones(k)
    levels = np.array([10, -10, 5, -5, 0])
    a = np.random.permutation(np.resize(levels, k // 512 * 4)).reshape(k // 512, 4)
    idx = np.arange(k)
    return np.exp2(a[idx // 512, idx % 128 // 32])


BF16 = ml_dtypes.bfloat16


def bf(x):
    return np.asarray(x, np.float32).astype(BF16)


def f64(x):
    return np.asarray(x).astype(np.float64)


NS, NT, DS, DT, DH, DB, DO, NF, SP = 512, 1024, 1024, 128, 1024, 1024, 512, 2, 16
EPS_ROW = 1e-8
EPS_BN = 1e-5


def row_norm(a):
    return a / np.maximum(a.sum(axis=1, keepdims=True), EPS_ROW)


def bn_eval(x, gamma, beta, mean, var):
    return (x - mean) * (gamma / np.sqrt(var + EPS_BN)) + beta


def setup_inputs():
    t = mx_kscale(DS)
    edges = np.random.random((NT, NS)) < 1.0 / SP
    linked = np.random.random((NT, 1)) > 0.03
    return {"H_source": bf(np.random.standard_normal((NS, DS)) * t),
            "A": bf(np.random.random((NT, NS)) * edges * linked),
            "W0": bf(np.random.standard_normal((DS, DH)) * np.sqrt(NS / SP / DS) / t[:, None]),
            "b0": bf(np.random.standard_normal(DH) * 0.1),
            "bn_gamma": bf(np.random.uniform(0.5, 1.5, DH)),
            "bn_beta": bf(np.random.standard_normal(DH) * 0.1),
            "bn_mean": bf(np.random.standard_normal(DH) * 0.1),
            "bn_var": bf(np.random.uniform(0.5, 1.5, DH))}


def reference(H_source, A, W0, b0, bn_gamma, bn_beta, bn_mean, bn_var):
    a_n = row_norm(f64(A))
    agg = mxq(a_n, 1, "e4m3") @ mxq(f64(H_source), 0, "e4m3")
    h = (mxq(agg, 1, "e4m3") @ mxq(f64(W0), 0, "e4m3")) + f64(b0)
    return np.maximum(bn_eval(h, f64(bn_gamma), f64(bn_beta), f64(bn_mean), f64(bn_var)), 0.0)

@@ -1,0 +1,252 @@
+from contextlib import ExitStack
+
+import concourse.mybir as mybir
+from concourse.masks import make_identity
+
+BF16 = mybir.dt.bfloat16
+F32 = mybir.dt.float32
+U32 = mybir.dt.uint32
+U8 = mybir.dt.uint8
+FP8X4 = mybir.dt.float8_e4m3fn_x4
+ACT = mybir.ActivationFunctionType
+ALU = mybir.AluOpType
+
+P = 128
+PACK = 4
+K_PASS = P * PACK
+
+NS, NT, DS, DH = 512, 1024, 1024, 1024
+EPS_ROW = 1e-8
+EPS_BN = 1e-5
+
+TB = NT // P
+HB = DH // P
+G = DS // K_PASS
+CHUNK_TB = 4
+CHUNKS = TB // CHUNK_TB
+CHUNK = CHUNK_TB * P
+HALF = 512
+
+FLOPS = 2 * NT * NS * DS + 2 * NT * DS * DH
+
+
+def tile_bipartitegcnstack_pa_kernel(
+    tc, H_source, A, W0, b0, bn_gamma, bn_beta, bn_mean, bn_var, out
+):
+    nc = tc.nc
+    with ExitStack() as ctx:
+        keep = ctx.enter_context(tc.tile_pool(name="keep", bufs=1))
+        scratch = ctx.enter_context(tc.tile_pool(name="scratch", bufs=2))
+        psum_tr = ctx.enter_context(tc.psum_pool(name="psum_tr", bufs=2))
+        psum_agg = ctx.enter_context(tc.psum_pool(name="psum_agg", bufs=3))
+        psum_h = ctx.enter_context(tc.psum_pool(name="psum_h", bufs=3))
+
+        a_raw = keep.tile([P, TB, NS], BF16)
+        a_norm = keep.tile([P, TB, NS], BF16)
+        a_grouped = keep.tile([P, TB, P, PACK], BF16, align_bytes=64)
+        a_codes = keep.tile([P, NT], U32, align_bytes=64)
+        a_scales = keep.tile([P, NT], U8, align_bytes=64)
+
+        h_raw = keep.tile([P, PACK, DS], BF16)
+        h_grouped = keep.tile([P, DS, PACK], BF16, align_bytes=64)
+        h_codes = keep.tile([P, DS], U32, align_bytes=64)
+        h_scales = keep.tile([P, DS], U8, align_bytes=64)
+
+        w_raw = keep.tile([P, G * PACK, DH], BF16)
+        w_grouped = keep.tile([P, G, DH, PACK], BF16, align_bytes=64)
+        w_codes = keep.tile([P, G, DH], U32, align_bytes=64)
+        w_scales = keep.tile([P, G, DH], U8, align_bytes=64)
+
+        agg_grouped = keep.tile([P, G, TB, P, PACK], BF16, align_bytes=64)
+        agg_codes = keep.tile([P, G, NT], U32, align_bytes=64)
+        agg_scales = keep.tile([P, G, NT], U8, align_bytes=64)
+
+        y_t = keep.tile([P, HB, NT], F32)
+        y = keep.tile([P, TB, DH], F32)
+
+        a_view = A.rearrange("(p tb) s -> p tb s", tb=TB)
+        w_view = W0.rearrange("(gj p) h -> p gj h", p=P)
+        out_view = out.rearrange("(p tb) h -> p tb h", tb=TB)
+        nc.sync.dma_start(out=a_raw[:, 0:2, :], in_=a_view[:, 0:2, :])
+        nc.sync.dma_start(out=a_raw[:, 2:4, :], in_=a_view[:, 2:4, :])
+        nc.sync.dma_start(out=h_raw[:], in_=H_source.rearrange("(j p) d -> p j d", p=P))
+        nc.sync.dma_start(out=a_raw[:, 4:8, :], in_=a_view[:, 4:8, :])
+        for half in range(DH // HALF):
+            cols = slice(half * HALF, (half + 1) * HALF)
+            nc.sync.dma_start(out=w_raw[:, :, cols], in_=w_view[:, :, cols])
+
+        warm = keep.tile([P, 1], F32)
+        nc.vector.memset(warm[:], 1.0)
+        nc.scalar.activation(out=warm[:], in_=warm[:], func=ACT.Sqrt)
+
+        ident_bf = keep.tile([P, P], BF16)
+        make_identity(nc, ident_bf[:])
+        ident_f32 = keep.tile([P, P], F32)
+        make_identity(nc, ident_f32[:])
+
+        vectors = [b0, bn_gamma, bn_beta, bn_mean, bn_var]
+        par_rows = keep.tile([P, P], BF16)
+        nc.gpsimd.memset(par_rows[:], 0.0)
+        for v, vector in enumerate(vectors):
+            nc.gpsimd.dma_start(
+                out=par_rows[v * HB : (v + 1) * HB, :],
+                in_=vector.rearrange("(hb c) -> hb c", c=P),
+            )
+        par_ps = psum_tr.tile([P, P], BF16, tag="tr")
+        nc.tensor.transpose(par_ps[:], par_rows[:], ident_bf[:])
+        par = keep.tile([P, len(vectors), HB], F32)
+        nc.vector.tensor_copy(
+            out=par[:].rearrange("p v hb -> p (v hb)"), in_=par_ps[:, 0 : len(vectors) * HB]
+        )
+        bias_c, gamma_c, beta_c, mean_c, var_c = [par[:, v, :] for v in range(len(vectors))]
+        std = keep.tile([P, HB], F32)
+        scale_c = keep.tile([P, HB], F32)
+        shift_c = keep.tile([P, HB], F32)
+        nc.vector.tensor_scalar_add(out=std[:], in0=var_c, scalar1=EPS_BN)
+        nc.scalar.activation(out=std[:], in_=std[:], func=ACT.Sqrt)
+        nc.vector.reciprocal(out=scale_c[:], in_=std[:])
+        nc.vector.tensor_mul(out=scale_c[:], in0=scale_c[:], in1=gamma_c)
+        nc.vector.tensor_sub(out=shift_c[:], in0=bias_c, in1=mean_c)
+        nc.vector.tensor_mul(out=shift_c[:], in0=shift_c[:], in1=scale_c[:])
+        nc.vector.tensor_add(out=shift_c[:], in0=shift_c[:], in1=beta_c)
+
+        row_sum = keep.tile([P, TB], F32)
+        row_inv = keep.tile([P, TB], F32)
+
+        def normalise_and_transpose(tb):
+            one = slice(tb, tb + 1)
+            unused = scratch.tile([P, NS], BF16)
+            nc.scalar.activation(
+                out=unused[:], in_=a_raw[:, tb, :], func=ACT.Copy, accum_out=row_sum[:, one]
+            )
+            nc.vector.tensor_scalar_max(out=row_inv[:, one], in0=row_sum[:, one], scalar1=EPS_ROW)
+            nc.vector.reciprocal(out=row_inv[:, one], in_=row_inv[:, one])
+            nc.vector.tensor_scalar_mul(
+                out=a_norm[:, tb, :], in0=a_raw[:, tb, :], scalar1=row_inv[:, one]
+            )
+            turned = psum_tr.tile([P, PACK, P], BF16, tag="tr")
+            for j in range(PACK):
+                nc.tensor.transpose(turned[:, j, :], a_norm[:, tb, j * P : (j + 1) * P], ident_bf[:])
+            nc.scalar.copy(out=a_grouped[:, tb, :, :], in_=turned[:].rearrange("p j t -> p t j"))
+
+        def quantise_a(chunk):
+            cols = slice(chunk * CHUNK, (chunk + 1) * CHUNK)
+            blocks = slice(chunk * CHUNK_TB, (chunk + 1) * CHUNK_TB)
+            nc.vector.quantize_mx(
+                out=a_codes[:, cols].bitcast(FP8X4),
+                scales=a_scales[:, cols],
+                in_=a_grouped[:, blocks, :, :].rearrange("p tb t j -> p (tb t j)"),
+            )
+
+        def regroup(grouped, rows):
+            nc.vector.tensor_copy(
+                out=grouped.rearrange("p (c i) j -> p c j i", i=4),
+                in_=rows.rearrange("p j (c i) -> p c j i", i=4),
+            )
+
+        def quantise(codes, scales, grouped):
+            nc.vector.quantize_mx(
+                out=codes.bitcast(FP8X4), scales=scales, in_=grouped.rearrange("p c j -> p (c j)")
+            )
+
+        def quantise_h_source():
+            halves = [slice(i * HALF, (i + 1) * HALF) for i in range(DS // HALF)]
+            for cols in halves:
+                regroup(h_grouped[:, cols, :], h_raw[:, :, cols])
+            for cols in halves:
+                quantise(h_codes[:, cols], h_scales[:, cols], h_grouped[:, cols, :])
+
+        def quantise_w(half):
+            cols = slice(half * HALF, (half + 1) * HALF)
+            for g in range(G):
+                regroup(w_grouped[:, g, cols, :], w_raw[:, g * PACK : (g + 1) * PACK, cols])
+            for g in range(G):
+                quantise(w_codes[:, g, cols], w_scales[:, g, cols], w_grouped[:, g, cols, :])
+
+        def aggregate(tb):
+            t_cols = slice(tb * P, (tb + 1) * P)
+            for g in range(G):
+                acc = psum_agg.tile([P, PACK, P], F32)
+                for j in range(PACK):
+                    d_cols = slice((g * PACK + j) * P, (g * PACK + j + 1) * P)
+                    nc.tensor.matmul_mx(
+                        out=acc[:, j, :],
+                        lhsT=h_codes[:, d_cols].bitcast(FP8X4),
+                        lhsT_scale=h_scales[:, d_cols],
+                        rhs=a_codes[:, t_cols].bitcast(FP8X4),
+                        rhs_scale=a_scales[:, t_cols],
+                        start=True,
+                        stop=True,
+                    )
+                nc.scalar.copy(out=agg_grouped[:, g, tb, :, :], in_=acc[:].rearrange("p j t -> p t j"))
+
+        def quantise_agg(chunk):
+            cols = slice(chunk * CHUNK, (chunk + 1) * CHUNK)
+            blocks = slice(chunk * CHUNK_TB, (chunk + 1) * CHUNK_TB)
+            for g in range(G):
+                nc.vector.quantize_mx(
+                    out=agg_codes[:, g, cols].bitcast(FP8X4),
+                    scales=agg_scales[:, g, cols],
+                    in_=agg_grouped[:, g, blocks, :, :].rearrange("p tb t j -> p (tb t j)"),
+                )
+
+        def linear_bn_relu(chunk, hb):
+            t_cols = slice(chunk * CHUNK, (chunk + 1) * CHUNK)
+            h_cols = slice(hb * P, (hb + 1) * P)
+            acc = psum_h.tile([P, CHUNK], F32)
+            for g in range(G):
+                nc.tensor.matmul_mx(
+                    out=acc[:],
+                    lhsT=w_codes[:, g, h_cols].bitcast(FP8X4),
+                    lhsT_scale=w_scales[:, g, h_cols],
+                    rhs=agg_codes[:, g, t_cols].bitcast(FP8X4),
+                    rhs_scale=agg_scales[:, g, t_cols],
+                    start=(g == 0),
+                    stop=(g == G - 1),
+                )
+            nc.scalar.activation(
+                out=y_t[:, hb, t_cols],
+                in_=acc[:],
+                func=ACT.Relu,
+                bias=shift_c[:, hb : hb + 1],
+                scale=scale_c[:, hb : hb + 1],
+            )
+
+        def turn_back_and_store(tb):
+            for quad in range(HB // PACK):
+                turned = psum_tr.tile([P, PACK, P], F32, tag="tr")
+                for q in range(PACK):
+                    nc.tensor.transpose(
+                        turned[:, q, :], y_t[:, quad * PACK + q, tb * P : (tb + 1) * P], ident_f32[:]
+                    )
+                nc.vector.tensor_copy(
+                    out=y[:, tb, quad * PACK * P : (quad + 1) * PACK * P],
+                    in_=turned[:].rearrange("p q h -> p (q h)"),
+                )
+            nc.sync.dma_start(out=out_view[:, tb, :], in_=y[:, tb, :])
+
+        for tb in range(CHUNK_TB):
+            normalise_and_transpose(tb)
+        quantise_h_source()
+        quantise_a(0)
+        for tb in range(CHUNK_TB):
+            aggregate(tb)
+        quantise_w(0)
+        for tb in range(CHUNK_TB, TB):
+            normalise_and_transpose(tb)
+        quantise_a(1)
+        quantise_agg(0)
+        for hb in range(HB // 2):
+            linear_bn_relu(0, hb)
+        for tb in range(CHUNK_TB, TB):
+            aggregate(tb)
+        quantise_w(1)
+        for hb in range(HB // 2, HB):
+            linear_bn_relu(0, hb)
+        quantise_agg(1)
+        for tb in range(CHUNK_TB):
+            turn_back_and_store(tb)
+        for hb in range(HB):
+            linear_bn_relu(1, hb)
+        for tb in range(CHUNK_TB, TB):
+            turn_back_and_store(tb)

@@ -37,9 +37,7 @@ def tile_bipartitegcnstack_pa_kernel(
     with ExitStack() as ctx:
         keep = ctx.enter_context(tc.tile_pool(name="keep", bufs=1))
         scratch = ctx.enter_context(tc.tile_pool(name="scratch", bufs=2))
-        psum_tr = ctx.enter_context(tc.psum_pool(name="psum_tr", bufs=2))
-        psum_agg = ctx.enter_context(tc.psum_pool(name="psum_agg", bufs=3))
-        psum_h = ctx.enter_context(tc.psum_pool(name="psum_h", bufs=3))
+        psum = ctx.enter_context(tc.psum_pool(name="psum", bufs=8))
 
         a_raw = keep.tile([P, TB, NS], BF16)
         a_norm = keep.tile([P, TB, NS], BF16)
@@ -64,67 +62,68 @@ def tile_bipartitegcnstack_pa_kernel(
         y_t = keep.tile([P, HB, NT], F32)
         y = keep.tile([P, TB, DH], F32)
 
-        a_view = A.rearrange("(p tb) s -> p tb s", tb=TB)
-        w_view = W0.rearrange("(gj p) h -> p gj h", p=P)
-        out_view = out.rearrange("(p tb) h -> p tb h", tb=TB)
-        nc.sync.dma_start(out=a_raw[:, 0:2, :], in_=a_view[:, 0:2, :])
-        nc.sync.dma_start(out=a_raw[:, 2:4, :], in_=a_view[:, 2:4, :])
-        nc.sync.dma_start(out=h_raw[:], in_=H_source.rearrange("(j p) d -> p j d", p=P))
-        nc.sync.dma_start(out=a_raw[:, 4:8, :], in_=a_view[:, 4:8, :])
-        for half in range(DH // HALF):
-            cols = slice(half * HALF, (half + 1) * HALF)
-            nc.sync.dma_start(out=w_raw[:, :, cols], in_=w_view[:, :, cols])
-
-        warm = keep.tile([P, 1], F32)
-        nc.vector.memset(warm[:], 1.0)
-        nc.scalar.activation(out=warm[:], in_=warm[:], func=ACT.Sqrt)
-
-        ident_bf = keep.tile([P, P], BF16)
-        make_identity(nc, ident_bf[:])
-        ident_f32 = keep.tile([P, P], F32)
-        make_identity(nc, ident_f32[:])
-
         vectors = [b0, bn_gamma, bn_beta, bn_mean, bn_var]
         par_rows = keep.tile([P, P], BF16)
-        nc.gpsimd.memset(par_rows[:], 0.0)
-        for v, vector in enumerate(vectors):
-            nc.gpsimd.dma_start(
-                out=par_rows[v * HB : (v + 1) * HB, :],
-                in_=vector.rearrange("(hb c) -> hb c", c=P),
-            )
-        par_ps = psum_tr.tile([P, P], BF16, tag="tr")
-        nc.tensor.transpose(par_ps[:], par_rows[:], ident_bf[:])
         par = keep.tile([P, len(vectors), HB], F32)
-        nc.vector.tensor_copy(
-            out=par[:].rearrange("p v hb -> p (v hb)"), in_=par_ps[:, 0 : len(vectors) * HB]
-        )
         bias_c, gamma_c, beta_c, mean_c, var_c = [par[:, v, :] for v in range(len(vectors))]
         std = keep.tile([P, HB], F32)
         scale_c = keep.tile([P, HB], F32)
         shift_c = keep.tile([P, HB], F32)
-        nc.vector.tensor_scalar_add(out=std[:], in0=var_c, scalar1=EPS_BN)
-        nc.scalar.activation(out=std[:], in_=std[:], func=ACT.Sqrt)
-        nc.vector.reciprocal(out=scale_c[:], in_=std[:])
-        nc.vector.tensor_mul(out=scale_c[:], in0=scale_c[:], in1=gamma_c)
-        nc.vector.tensor_sub(out=shift_c[:], in0=bias_c, in1=mean_c)
-        nc.vector.tensor_mul(out=shift_c[:], in0=shift_c[:], in1=scale_c[:])
-        nc.vector.tensor_add(out=shift_c[:], in0=shift_c[:], in1=beta_c)
 
         row_sum = keep.tile([P, TB], F32)
         row_inv = keep.tile([P, TB], F32)
+        warm = keep.tile([P, 1], F32)
+        ident_bf = keep.tile([P, P], BF16)
+        ident_f32 = keep.tile([P, P], F32)
 
-        def normalise_and_transpose(tb):
-            one = slice(tb, tb + 1)
-            unused = scratch.tile([P, NS], BF16)
-            nc.scalar.activation(
-                out=unused[:], in_=a_raw[:, tb, :], func=ACT.Copy, accum_out=row_sum[:, one]
-            )
-            nc.vector.tensor_scalar_max(out=row_inv[:, one], in0=row_sum[:, one], scalar1=EPS_ROW)
-            nc.vector.reciprocal(out=row_inv[:, one], in_=row_inv[:, one])
-            nc.vector.tensor_scalar_mul(
-                out=a_norm[:, tb, :], in0=a_raw[:, tb, :], scalar1=row_inv[:, one]
-            )
-            turned = psum_tr.tile([P, PACK, P], BF16, tag="tr")
+        a_view = A.rearrange("(p tb) s -> p tb s", tb=TB)
+        w_view = W0.rearrange("(gj p) h -> p gj h", p=P)
+        out_view = out.rearrange("(p tb) h -> p tb h", tb=TB)
+
+        def load_everything():
+            nc.vector.memset(par_rows[:], 0.0)
+            nc.sync.dma_start(out=a_raw[:, 0:2, :], in_=a_view[:, 0:2, :])
+            nc.sync.dma_start(out=a_raw[:, 2:4, :], in_=a_view[:, 2:4, :])
+            nc.sync.dma_start(out=a_raw[:, 4:8, :], in_=a_view[:, 4:8, :])
+            nc.sync.dma_start(out=h_raw[:], in_=H_source.rearrange("(j p) d -> p j d", p=P))
+            for v, vector in enumerate(vectors):
+                nc.sync.dma_start(
+                    out=par_rows[v * HB : (v + 1) * HB, :],
+                    in_=vector.rearrange("(hb c) -> hb c", c=P),
+                )
+            for half in range(DH // HALF):
+                cols = slice(half * HALF, (half + 1) * HALF)
+                nc.sync.dma_start(out=w_raw[:, :, cols], in_=w_view[:, :, cols])
+
+        def constants():
+            nc.vector.memset(warm[:], 1.0)
+            nc.scalar.activation(out=warm[:], in_=warm[:], func=ACT.Sqrt)
+            make_identity(nc, ident_bf[:])
+            make_identity(nc, ident_f32[:])
+
+        def normalise(chunk):
+            blocks = range(chunk * CHUNK_TB, (chunk + 1) * CHUNK_TB)
+            four = slice(chunk * CHUNK_TB, (chunk + 1) * CHUNK_TB)
+            for tb in blocks:
+                unused = scratch.tile([P, NS], BF16)
+                nc.vector.tensor_scalar(
+                    out=unused[:],
+                    in0=a_raw[:, tb, :],
+                    scalar1=1.0,
+                    scalar2=None,
+                    op0=ALU.mult,
+                    op1=ALU.add,
+                    accum_out=row_sum[:, tb : tb + 1],
+                )
+            nc.vector.tensor_scalar_max(out=row_inv[:, four], in0=row_sum[:, four], scalar1=EPS_ROW)
+            nc.vector.reciprocal(out=row_inv[:, four], in_=row_inv[:, four])
+            for tb in blocks:
+                nc.vector.tensor_scalar_mul(
+                    out=a_norm[:, tb, :], in0=a_raw[:, tb, :], scalar1=row_inv[:, tb : tb + 1]
+                )
+
+        def transpose_a(tb):
+            turned = psum.tile([P, PACK, P], BF16, tag="bank")
             for j in range(PACK):
                 nc.tensor.transpose(turned[:, j, :], a_norm[:, tb, j * P : (j + 1) * P], ident_bf[:])
             nc.scalar.copy(out=a_grouped[:, tb, :, :], in_=turned[:].rearrange("p j t -> p t j"))
@@ -149,24 +148,46 @@ def tile_bipartitegcnstack_pa_kernel(
                 out=codes.bitcast(FP8X4), scales=scales, in_=grouped.rearrange("p c j -> p (c j)")
             )
 
-        def quantise_h_source():
-            halves = [slice(i * HALF, (i + 1) * HALF) for i in range(DS // HALF)]
-            for cols in halves:
+        def regroup_h_source():
+            for half in range(DS // HALF):
+                cols = slice(half * HALF, (half + 1) * HALF)
                 regroup(h_grouped[:, cols, :], h_raw[:, :, cols])
-            for cols in halves:
+
+        def quantise_h_source():
+            for half in range(DS // HALF):
+                cols = slice(half * HALF, (half + 1) * HALF)
                 quantise(h_codes[:, cols], h_scales[:, cols], h_grouped[:, cols, :])
+
+        def regroup_w(half):
+            cols = slice(half * HALF, (half + 1) * HALF)
+            for g in range(G):
+                regroup(w_grouped[:, g, cols, :], w_raw[:, g * PACK : (g + 1) * PACK, cols])
 
         def quantise_w(half):
             cols = slice(half * HALF, (half + 1) * HALF)
             for g in range(G):
-                regroup(w_grouped[:, g, cols, :], w_raw[:, g * PACK : (g + 1) * PACK, cols])
-            for g in range(G):
                 quantise(w_codes[:, g, cols], w_scales[:, g, cols], w_grouped[:, g, cols, :])
+
+        def turn_vectors():
+            par_ps = psum.tile([P, P], BF16, tag="bank")
+            nc.tensor.transpose(par_ps[:], par_rows[:], ident_bf[:])
+            nc.vector.tensor_copy(
+                out=par[:].rearrange("p v hb -> p (v hb)"), in_=par_ps[:, 0 : len(vectors) * HB]
+            )
+            nc.vector.tensor_scalar_add(out=std[:], in0=var_c, scalar1=EPS_BN)
+            nc.scalar.activation(out=std[:], in_=std[:], func=ACT.Sqrt)
+
+        def scale_and_shift():
+            nc.vector.reciprocal(out=scale_c[:], in_=std[:])
+            nc.vector.tensor_mul(out=scale_c[:], in0=scale_c[:], in1=gamma_c)
+            nc.vector.tensor_sub(out=shift_c[:], in0=bias_c, in1=mean_c)
+            nc.vector.tensor_mul(out=shift_c[:], in0=shift_c[:], in1=scale_c[:])
+            nc.vector.tensor_add(out=shift_c[:], in0=shift_c[:], in1=beta_c)
 
         def aggregate(tb):
             t_cols = slice(tb * P, (tb + 1) * P)
             for g in range(G):
-                acc = psum_agg.tile([P, PACK, P], F32)
+                acc = psum.tile([P, PACK, P], F32, tag="bank")
                 for j in range(PACK):
                     d_cols = slice((g * PACK + j) * P, (g * PACK + j + 1) * P)
                     nc.tensor.matmul_mx(
@@ -190,63 +211,68 @@ def tile_bipartitegcnstack_pa_kernel(
                     in_=agg_grouped[:, g, blocks, :, :].rearrange("p tb t j -> p (tb t j)"),
                 )
 
-        def linear_bn_relu(chunk, hb):
+        def linear_bn_relu(chunk, quad):
             t_cols = slice(chunk * CHUNK, (chunk + 1) * CHUNK)
-            h_cols = slice(hb * P, (hb + 1) * P)
-            acc = psum_h.tile([P, CHUNK], F32)
-            for g in range(G):
-                nc.tensor.matmul_mx(
-                    out=acc[:],
-                    lhsT=w_codes[:, g, h_cols].bitcast(FP8X4),
-                    lhsT_scale=w_scales[:, g, h_cols],
-                    rhs=agg_codes[:, g, t_cols].bitcast(FP8X4),
-                    rhs_scale=agg_scales[:, g, t_cols],
-                    start=(g == 0),
-                    stop=(g == G - 1),
+            for hb in range(quad * PACK, (quad + 1) * PACK):
+                h_cols = slice(hb * P, (hb + 1) * P)
+                acc = psum.tile([P, CHUNK], F32, tag="bank")
+                for g in range(G):
+                    nc.tensor.matmul_mx(
+                        out=acc[:],
+                        lhsT=w_codes[:, g, h_cols].bitcast(FP8X4),
+                        lhsT_scale=w_scales[:, g, h_cols],
+                        rhs=agg_codes[:, g, t_cols].bitcast(FP8X4),
+                        rhs_scale=agg_scales[:, g, t_cols],
+                        start=(g == 0),
+                        stop=(g == G - 1),
+                    )
+                nc.scalar.activation(
+                    out=y_t[:, hb, t_cols],
+                    in_=acc[:],
+                    func=ACT.Relu,
+                    bias=shift_c[:, hb : hb + 1],
+                    scale=scale_c[:, hb : hb + 1],
                 )
-            nc.scalar.activation(
-                out=y_t[:, hb, t_cols],
-                in_=acc[:],
-                func=ACT.Relu,
-                bias=shift_c[:, hb : hb + 1],
-                scale=scale_c[:, hb : hb + 1],
-            )
 
-        def turn_back_and_store(tb):
-            for quad in range(HB // PACK):
-                turned = psum_tr.tile([P, PACK, P], F32, tag="tr")
+        def turn_back_and_store(chunk, quad):
+            h_cols = slice(quad * PACK * P, (quad + 1) * PACK * P)
+            for tb in range(chunk * CHUNK_TB, (chunk + 1) * CHUNK_TB):
+                turned = psum.tile([P, PACK, P], F32, tag="bank")
                 for q in range(PACK):
                     nc.tensor.transpose(
                         turned[:, q, :], y_t[:, quad * PACK + q, tb * P : (tb + 1) * P], ident_f32[:]
                     )
-                nc.vector.tensor_copy(
-                    out=y[:, tb, quad * PACK * P : (quad + 1) * PACK * P],
-                    in_=turned[:].rearrange("p q h -> p (q h)"),
-                )
-            nc.sync.dma_start(out=out_view[:, tb, :], in_=y[:, tb, :])
+                nc.vector.tensor_copy(out=y[:, tb, h_cols], in_=turned[:].rearrange("p q h -> p (q h)"))
+                nc.sync.dma_start(out=out_view[:, tb, h_cols], in_=y[:, tb, h_cols])
 
-        for tb in range(CHUNK_TB):
-            normalise_and_transpose(tb)
-        quantise_h_source()
-        quantise_a(0)
-        for tb in range(CHUNK_TB):
-            aggregate(tb)
-        quantise_w(0)
-        for tb in range(CHUNK_TB, TB):
-            normalise_and_transpose(tb)
-        quantise_a(1)
-        quantise_agg(0)
-        for hb in range(HB // 2):
-            linear_bn_relu(0, hb)
-        for tb in range(CHUNK_TB, TB):
-            aggregate(tb)
-        quantise_w(1)
-        for hb in range(HB // 2, HB):
-            linear_bn_relu(0, hb)
-        quantise_agg(1)
-        for tb in range(CHUNK_TB):
-            turn_back_and_store(tb)
-        for hb in range(HB):
-            linear_bn_relu(1, hb)
-        for tb in range(CHUNK_TB, TB):
-            turn_back_and_store(tb)
+        with tc.manual_schedule():
+            load_everything()
+            constants()
+            for chunk in range(CHUNKS):
+                normalise(chunk)
+                for tb in range(chunk * CHUNK_TB, (chunk + 1) * CHUNK_TB):
+                    transpose_a(tb)
+            regroup_h_source()
+            quantise_a(0)
+            turn_vectors()
+            quantise_h_source()
+            quantise_a(1)
+            for tb in range(CHUNK_TB):
+                aggregate(tb)
+            regroup_w(0)
+            scale_and_shift()
+            quantise_w(0)
+            quantise_agg(0)
+            for tb in range(CHUNK_TB, TB):
+                aggregate(tb)
+            linear_bn_relu(0, 0)
+            regroup_w(1)
+            quantise_w(1)
+            quantise_agg(1)
+            linear_bn_relu(0, 1)
+            turn_back_and_store(0, 0)
+            linear_bn_relu(1, 0)
+            turn_back_and_store(0, 1)
+            linear_bn_relu(1, 1)
+            turn_back_and_store(1, 0)
+            turn_back_and_store(1, 1)

@@ -14,6 +14,8 @@ ALU = mybir.AluOpType
 P = 128
 PACK = 4
 K_PASS = P * PACK
+BLK = 32
+QUADS = P // BLK
 
 NS, NT, DS, DH = 512, 1024, 1024, 1024
 EPS_ROW = 1e-8
@@ -22,10 +24,11 @@ EPS_BN = 1e-5
 TB = NT // P
 HB = DH // P
 G = DS // K_PASS
-CHUNK_TB = 4
-CHUNKS = TB // CHUNK_TB
-CHUNK = CHUNK_TB * P
 HALF = 512
+HQ = HB // 2
+PAIR = 2
+V_TB = 6
+JB = P // BLK
 
 FLOPS = 2 * NT * NS * DS + 2 * NT * DS * DH
 
@@ -51,7 +54,7 @@ def tile_bipartitegcnstack_pa_kernel(
         h_scales = keep.tile([P, DS], U8, align_bytes=64)
 
         w_raw = keep.tile([P, G * PACK, DH], BF16)
-        w_grouped = keep.tile([P, G, DH, PACK], BF16, align_bytes=64)
+        w_grouped = keep.tile([P, G, HB, P, PACK], BF16, align_bytes=64)
         w_codes = keep.tile([P, G, DH], U32, align_bytes=64)
         w_scales = keep.tile([P, G, DH], U8, align_bytes=64)
 
@@ -59,8 +62,10 @@ def tile_bipartitegcnstack_pa_kernel(
         agg_codes = keep.tile([P, G, NT], U32, align_bytes=64)
         agg_scales = keep.tile([P, G, NT], U8, align_bytes=64)
 
-        y_t = keep.tile([P, HB, NT], F32)
-        y = keep.tile([P, TB, DH], F32)
+        y_t = keep.tile([P, 2, V_TB * JB, HQ, BLK], F32, align_bytes=64)
+        y_v = keep.tile([P, 2, V_TB * JB, HQ, BLK], F32, align_bytes=64)
+        y_p = keep.tile([P, HB, (TB - V_TB) * P], F32)
+        y_o = keep.tile([P, TB - V_TB, QUADS, HB, BLK], F32)
 
         vectors = [b0, bn_gamma, bn_beta, bn_mean, bn_var]
         par_rows = keep.tile([P, P], BF16)
@@ -76,203 +81,310 @@ def tile_bipartitegcnstack_pa_kernel(
         ident_bf = keep.tile([P, P], BF16)
         ident_f32 = keep.tile([P, P], F32)
 
-        a_view = A.rearrange("(p tb) s -> p tb s", tb=TB)
+        a_view = A.rearrange("(tb p) s -> p tb s", p=P)
+        h_view = H_source.rearrange("(p j) d -> p j d", j=PACK)
         w_view = W0.rearrange("(gj p) h -> p gj h", p=P)
-        out_view = out.rearrange("(p tb) h -> p tb h", tb=TB)
 
         def load_everything():
             nc.vector.memset(par_rows[:], 0.0)
-            nc.sync.dma_start(out=a_raw[:, 0:2, :], in_=a_view[:, 0:2, :])
-            nc.sync.dma_start(out=a_raw[:, 2:4, :], in_=a_view[:, 2:4, :])
-            nc.sync.dma_start(out=a_raw[:, 4:8, :], in_=a_view[:, 4:8, :])
-            nc.sync.dma_start(out=h_raw[:], in_=H_source.rearrange("(j p) d -> p j d", p=P))
+
+            def load_a(t0, t1):
+                nc.sync.dma_start(out=a_raw[:, t0:t1, :], in_=a_view[:, t0:t1, :])
+
+            def load_h(half):
+                cols = slice(half * HALF, (half + 1) * HALF)
+                nc.sync.dma_start(out=h_raw[:, :, cols], in_=h_view[:, :, cols])
+
+            def load_w(g):
+                js = slice(g * PACK, (g + 1) * PACK)
+                nc.sync.dma_start(out=w_raw[:, js, :], in_=w_view[:, js, :])
+
+            load_a(0, 2)
+            load_a(2, 4)
+            load_h(0)
+            load_a(4, 8)
+            load_h(1)
+            load_w(0)
             for v, vector in enumerate(vectors):
                 nc.sync.dma_start(
-                    out=par_rows[v * HB : (v + 1) * HB, :],
-                    in_=vector.rearrange("(hb c) -> hb c", c=P),
+                    out=par_rows[v * HB : (v + 1) * HB, :].rearrange("hb (i b) -> hb i b", b=BLK),
+                    in_=vector.rearrange("(i hb b) -> hb i b", hb=HB, b=BLK),
                 )
-            for half in range(DH // HALF):
-                cols = slice(half * HALF, (half + 1) * HALF)
-                nc.sync.dma_start(out=w_raw[:, :, cols], in_=w_view[:, :, cols])
+            load_w(1)
 
         def constants():
             nc.vector.memset(warm[:], 1.0)
             nc.scalar.activation(out=warm[:], in_=warm[:], func=ACT.Sqrt)
-            make_identity(nc, ident_bf[:])
             make_identity(nc, ident_f32[:])
+            make_identity(nc, ident_bf[:])
 
-        def normalise(chunk):
-            blocks = range(chunk * CHUNK_TB, (chunk + 1) * CHUNK_TB)
-            four = slice(chunk * CHUNK_TB, (chunk + 1) * CHUNK_TB)
-            for tb in blocks:
-                unused = scratch.tile([P, NS], BF16)
-                nc.vector.tensor_scalar(
-                    out=unused[:],
-                    in0=a_raw[:, tb, :],
-                    scalar1=1.0,
-                    scalar2=None,
-                    op0=ALU.mult,
-                    op1=ALU.add,
-                    accum_out=row_sum[:, tb : tb + 1],
-                )
-            nc.vector.tensor_scalar_max(out=row_inv[:, four], in0=row_sum[:, four], scalar1=EPS_ROW)
-            nc.vector.reciprocal(out=row_inv[:, four], in_=row_inv[:, four])
-            for tb in blocks:
-                nc.vector.tensor_scalar_mul(
-                    out=a_norm[:, tb, :], in0=a_raw[:, tb, :], scalar1=row_inv[:, tb : tb + 1]
-                )
+        def row_sum_vector(tb):
+            unused = scratch.tile([P, NS], BF16)
+            nc.vector.tensor_scalar(
+                out=unused[:],
+                in0=a_raw[:, tb, :],
+                scalar1=1.0,
+                scalar2=None,
+                op0=ALU.mult,
+                op1=ALU.add,
+                accum_out=row_sum[:, tb : tb + 1],
+            )
 
-        def transpose_a(tb):
-            turned = psum.tile([P, PACK, P], BF16, tag="bank")
-            for j in range(PACK):
-                nc.tensor.transpose(turned[:, j, :], a_norm[:, tb, j * P : (j + 1) * P], ident_bf[:])
-            nc.scalar.copy(out=a_grouped[:, tb, :, :], in_=turned[:].rearrange("p j t -> p t j"))
+        def row_sum_scalar(tb):
+            unused_s = scratch.tile([P, NS], BF16)
+            nc.scalar.activation(
+                out=unused_s[:], in_=a_raw[:, tb, :], func=ACT.Copy, accum_out=row_sum[:, tb : tb + 1]
+            )
 
-        def quantise_a(chunk):
-            cols = slice(chunk * CHUNK, (chunk + 1) * CHUNK)
-            blocks = slice(chunk * CHUNK_TB, (chunk + 1) * CHUNK_TB)
+        def clamp(t0, t1):
+            nc.vector.tensor_scalar_max(out=row_inv[:, t0:t1], in0=row_sum[:, t0:t1], scalar1=EPS_ROW)
+
+        def invert(t0, t1):
+            nc.vector.reciprocal(out=row_inv[:, t0:t1], in_=row_inv[:, t0:t1])
+
+        def normalise(tb):
+            nc.vector.tensor_scalar_mul(
+                out=a_norm[:, tb, :], in0=a_raw[:, tb, :], scalar1=row_inv[:, tb : tb + 1]
+            )
+
+        def transpose_a(tb0):
+            turned = psum.tile([P, PAIR, 2, P], F32, tag="bank")
+            for b in range(PAIR):
+                words = a_norm[:, tb0 + b, :].bitcast(F32)
+                for u in range(2):
+                    nc.tensor.transpose(turned[:, b, u, :], words[:, u::2], ident_f32[:])
+            nc.scalar.copy(
+                out=a_grouped[:, tb0 : tb0 + PAIR, :, :].bitcast(F32),
+                in_=turned[:].rearrange("p b u t -> p b t u"),
+            )
+
+        def quantise_a(tb0):
+            cols = slice(tb0 * P, (tb0 + PAIR) * P)
             nc.vector.quantize_mx(
                 out=a_codes[:, cols].bitcast(FP8X4),
                 scales=a_scales[:, cols],
-                in_=a_grouped[:, blocks, :, :].rearrange("p tb t j -> p (tb t j)"),
+                in_=a_grouped[:, tb0 : tb0 + PAIR, :, :].rearrange("p tb t j -> p (tb t j)"),
             )
 
-        def regroup(grouped, rows):
+        def regroup_h(half):
+            cols = slice(half * HALF, (half + 1) * HALF)
             nc.vector.tensor_copy(
-                out=grouped.rearrange("p (c i) j -> p c j i", i=4),
-                in_=rows.rearrange("p j (c i) -> p c j i", i=4),
+                out=h_grouped[:, cols, :].rearrange("p (c i) j -> p c j i", i=4),
+                in_=h_raw[:, :, cols].rearrange("p j (c i) -> p c j i", i=4),
             )
 
-        def quantise(codes, scales, grouped):
+        def quantise_h(half):
+            cols = slice(half * HALF, (half + 1) * HALF)
             nc.vector.quantize_mx(
-                out=codes.bitcast(FP8X4), scales=scales, in_=grouped.rearrange("p c j -> p (c j)")
+                out=h_codes[:, cols].bitcast(FP8X4),
+                scales=h_scales[:, cols],
+                in_=h_grouped[:, cols, :].rearrange("p c j -> p (c j)"),
             )
 
-        def regroup_h_source():
-            for half in range(DS // HALF):
-                cols = slice(half * HALF, (half + 1) * HALF)
-                regroup(h_grouped[:, cols, :], h_raw[:, :, cols])
+        def regroup_w(g, half):
+            for hb in range(half * HB // 2, (half + 1) * HB // 2):
+                nc.vector.tensor_copy(
+                    out=w_grouped[:, g, hb, :, :].rearrange("p (i c k) j -> p i c j k", i=QUADS, k=4),
+                    in_=w_raw[:, g * PACK : (g + 1) * PACK, :].rearrange(
+                        "p j (i hb c k) -> p hb i c j k", i=QUADS, hb=HB, k=4
+                    )[:, hb],
+                )
 
-        def quantise_h_source():
-            for half in range(DS // HALF):
-                cols = slice(half * HALF, (half + 1) * HALF)
-                quantise(h_codes[:, cols], h_scales[:, cols], h_grouped[:, cols, :])
-
-        def regroup_w(half):
+        def quantise_w(g, half):
             cols = slice(half * HALF, (half + 1) * HALF)
-            for g in range(G):
-                regroup(w_grouped[:, g, cols, :], w_raw[:, g * PACK : (g + 1) * PACK, cols])
-
-        def quantise_w(half):
-            cols = slice(half * HALF, (half + 1) * HALF)
-            for g in range(G):
-                quantise(w_codes[:, g, cols], w_scales[:, g, cols], w_grouped[:, g, cols, :])
+            hbs = slice(half * HB // 2, (half + 1) * HB // 2)
+            nc.vector.quantize_mx(
+                out=w_codes[:, g, cols].bitcast(FP8X4),
+                scales=w_scales[:, g, cols],
+                in_=w_grouped[:, g, hbs, :, :].rearrange("p hb m j -> p (hb m j)"),
+            )
 
         def turn_vectors():
             par_ps = psum.tile([P, P], BF16, tag="bank")
             nc.tensor.transpose(par_ps[:], par_rows[:], ident_bf[:])
-            nc.vector.tensor_copy(
-                out=par[:].rearrange("p v hb -> p (v hb)"), in_=par_ps[:, 0 : len(vectors) * HB]
-            )
-            nc.vector.tensor_scalar_add(out=std[:], in0=var_c, scalar1=EPS_BN)
+            nc.scalar.copy(out=par[:].rearrange("p v hb -> p (v hb)"), in_=par_ps[:, 0 : len(vectors) * HB])
+            nc.gpsimd.tensor_scalar_add(out=std[:], in0=var_c, scalar1=EPS_BN)
             nc.scalar.activation(out=std[:], in_=std[:], func=ACT.Sqrt)
 
         def scale_and_shift():
             nc.vector.reciprocal(out=scale_c[:], in_=std[:])
-            nc.vector.tensor_mul(out=scale_c[:], in0=scale_c[:], in1=gamma_c)
-            nc.vector.tensor_sub(out=shift_c[:], in0=bias_c, in1=mean_c)
-            nc.vector.tensor_mul(out=shift_c[:], in0=shift_c[:], in1=scale_c[:])
-            nc.vector.tensor_add(out=shift_c[:], in0=shift_c[:], in1=beta_c)
+            nc.gpsimd.tensor_mul(out=scale_c[:], in0=scale_c[:], in1=gamma_c)
+            nc.gpsimd.tensor_sub(out=shift_c[:], in0=bias_c, in1=mean_c)
+            nc.gpsimd.tensor_mul(out=shift_c[:], in0=shift_c[:], in1=scale_c[:])
+            nc.gpsimd.tensor_add(out=shift_c[:], in0=shift_c[:], in1=beta_c)
 
-        def aggregate(tb):
+        def aggregate(g, tb, on_vector=False):
             t_cols = slice(tb * P, (tb + 1) * P)
-            for g in range(G):
-                acc = psum.tile([P, PACK, P], F32, tag="bank")
-                for j in range(PACK):
-                    d_cols = slice((g * PACK + j) * P, (g * PACK + j + 1) * P)
-                    nc.tensor.matmul_mx(
-                        out=acc[:, j, :],
-                        lhsT=h_codes[:, d_cols].bitcast(FP8X4),
-                        lhsT_scale=h_scales[:, d_cols],
-                        rhs=a_codes[:, t_cols].bitcast(FP8X4),
-                        rhs_scale=a_scales[:, t_cols],
-                        start=True,
-                        stop=True,
-                    )
-                nc.scalar.copy(out=agg_grouped[:, g, tb, :, :], in_=acc[:].rearrange("p j t -> p t j"))
-
-        def quantise_agg(chunk):
-            cols = slice(chunk * CHUNK, (chunk + 1) * CHUNK)
-            blocks = slice(chunk * CHUNK_TB, (chunk + 1) * CHUNK_TB)
-            for g in range(G):
-                nc.vector.quantize_mx(
-                    out=agg_codes[:, g, cols].bitcast(FP8X4),
-                    scales=agg_scales[:, g, cols],
-                    in_=agg_grouped[:, g, blocks, :, :].rearrange("p tb t j -> p (tb t j)"),
+            acc = psum.tile([P, PACK, P], F32, tag="bank")
+            for j in range(PACK):
+                d_cols = slice((g * PACK + j) * P, (g * PACK + j + 1) * P)
+                nc.tensor.matmul_mx(
+                    out=acc[:, j, :],
+                    lhsT=h_codes[:, d_cols].bitcast(FP8X4),
+                    lhsT_scale=h_scales[:, d_cols],
+                    rhs=a_codes[:, t_cols].bitcast(FP8X4),
+                    rhs_scale=a_scales[:, t_cols],
+                    start=True,
+                    stop=True,
                 )
+            src = acc[:].rearrange("p j t -> p t j")
+            if on_vector:
+                nc.vector.tensor_copy(out=agg_grouped[:, g, tb, :, :], in_=src)
+            else:
+                nc.scalar.copy(out=agg_grouped[:, g, tb, :, :], in_=src)
 
-        def linear_bn_relu(chunk, quad):
-            t_cols = slice(chunk * CHUNK, (chunk + 1) * CHUNK)
-            for hb in range(quad * PACK, (quad + 1) * PACK):
-                h_cols = slice(hb * P, (hb + 1) * P)
-                acc = psum.tile([P, CHUNK], F32, tag="bank")
+        def quantise_agg(g, tb0, n=PAIR):
+            cols = slice(tb0 * P, (tb0 + n) * P)
+            nc.vector.quantize_mx(
+                out=agg_codes[:, g, cols].bitcast(FP8X4),
+                scales=agg_scales[:, g, cols],
+                in_=agg_grouped[:, g, tb0 : tb0 + n, :, :].rearrange("p tb t j -> p (tb t j)"),
+            )
+
+        def linear_bn_relu(tb0, n, hb0, hb1):
+            t_cols = slice(tb0 * P, (tb0 + n) * P)
+            for hb in range(hb0, hb1):
+                m_cols = slice(hb * P, (hb + 1) * P)
+                acc = psum.tile([P, n * P], F32, tag="bank")
                 for g in range(G):
                     nc.tensor.matmul_mx(
                         out=acc[:],
-                        lhsT=w_codes[:, g, h_cols].bitcast(FP8X4),
-                        lhsT_scale=w_scales[:, g, h_cols],
+                        lhsT=w_codes[:, g, m_cols].bitcast(FP8X4),
+                        lhsT_scale=w_scales[:, g, m_cols],
                         rhs=agg_codes[:, g, t_cols].bitcast(FP8X4),
                         rhs_scale=agg_scales[:, g, t_cols],
                         start=(g == 0),
                         stop=(g == G - 1),
                     )
+                if tb0 < V_TB:
+                    dst = y_t[:, hb // HQ, tb0 * JB : (tb0 + n) * JB, hb % HQ, :]
+                    src = acc[:].rearrange("p (j a) -> p j a", a=BLK)
+                else:
+                    dst = y_p[:, hb, (tb0 - V_TB) * P : (tb0 - V_TB + n) * P]
+                    src = acc[:]
                 nc.scalar.activation(
-                    out=y_t[:, hb, t_cols],
-                    in_=acc[:],
+                    out=dst,
+                    in_=src,
                     func=ACT.Relu,
                     bias=shift_c[:, hb : hb + 1],
                     scale=scale_c[:, hb : hb + 1],
                 )
 
-        def turn_back_and_store(chunk, quad):
-            h_cols = slice(quad * PACK * P, (quad + 1) * PACK * P)
-            for tb in range(chunk * CHUNK_TB, (chunk + 1) * CHUNK_TB):
-                turned = psum.tile([P, PACK, P], F32, tag="bank")
-                for q in range(PACK):
+        def turn_back_vector(tb, n, half):
+            js = slice(tb * JB, (tb + n) * JB)
+            nc.vector.transpose(
+                y_v[:, half, js, :, :].rearrange("p j hb b -> p (j hb b)"),
+                y_t[:, half, js, :, :].rearrange("p j hb a -> p (j hb a)"),
+            )
+
+        def store_vector(tb0, n, half):
+            js = slice(tb0 * JB, (tb0 + n) * JB)
+            rows = out[tb0 * P : (tb0 + n) * P, :].rearrange("(j a) (i x c) -> i x a j c", a=BLK, i=QUADS, x=2)
+            for i in (0, 2, 1, 3):
+                nc.sync.dma_start(
+                    out=rows[i, half],
+                    in_=y_v[i * BLK : (i + 1) * BLK, half, js, :, :].rearrange("p j hb b -> p j (hb b)"),
+                )
+
+        def turn_back_tensor(tb):
+            x = tb - V_TB
+            for half in range(2):
+                turned = psum.tile([P, HB // 2, P], F32, tag="bank")
+                for q in range(HB // 2):
                     nc.tensor.transpose(
-                        turned[:, q, :], y_t[:, quad * PACK + q, tb * P : (tb + 1) * P], ident_f32[:]
+                        turned[:, q, :], y_p[:, half * HB // 2 + q, x * P : (x + 1) * P], ident_f32[:]
                     )
-                nc.vector.tensor_copy(out=y[:, tb, h_cols], in_=turned[:].rearrange("p q h -> p (q h)"))
-                nc.sync.dma_start(out=out_view[:, tb, h_cols], in_=y[:, tb, h_cols])
+                dst = y_o[:, x, :, half * HB // 2 : (half + 1) * HB // 2, :].rearrange("p i q b -> p q i b")
+                src = turned[:].rearrange("p q (i b) -> p q i b", b=BLK)
+                if half == 0:
+                    nc.scalar.copy(out=dst, in_=src)
+                else:
+                    nc.vector.tensor_copy(out=dst, in_=src)
+            nc.sync.dma_start(
+                out=out[tb * P : (tb + 1) * P, :], in_=y_o[:, x].rearrange("p i hb b -> p (i hb b)")
+            )
 
         with tc.manual_schedule():
             load_everything()
             constants()
-            for chunk in range(CHUNKS):
-                normalise(chunk)
-                for tb in range(chunk * CHUNK_TB, (chunk + 1) * CHUNK_TB):
-                    transpose_a(tb)
-            regroup_h_source()
+            row_sum_vector(0)
+            row_sum_scalar(1)
+            row_sum_scalar(3)
+            row_sum_vector(2)
+            clamp(0, 2)
+            invert(0, 2)
+            normalise(0)
+            normalise(1)
+            transpose_a(0)
+            clamp(2, 4)
+            invert(2, 4)
+            normalise(2)
+            normalise(3)
+            transpose_a(2)
+            regroup_h(0)
+            row_sum_scalar(5)
+            row_sum_scalar(6)
             quantise_a(0)
+            quantise_h(0)
+            quantise_a(2)
+            for tb in range(4):
+                aggregate(0, tb)
+            regroup_h(1)
+            row_sum_vector(4)
+            quantise_h(1)
+            row_sum_vector(7)
+            clamp(4, 8)
+
+            invert(4, 8)
+            for tb in range(4, TB):
+                normalise(tb)
+            for tb in range(2):
+                aggregate(1, tb)
+            transpose_a(4)
+            transpose_a(6)
             turn_vectors()
-            quantise_h_source()
-            quantise_a(1)
-            for tb in range(CHUNK_TB):
-                aggregate(tb)
-            regroup_w(0)
+            for tb in range(2, 4):
+                aggregate(1, tb)
+            regroup_w(0, 0)
+            quantise_a(4)
+            quantise_a(6)
             scale_and_shift()
-            quantise_w(0)
-            quantise_agg(0)
-            for tb in range(CHUNK_TB, TB):
-                aggregate(tb)
-            linear_bn_relu(0, 0)
-            regroup_w(1)
-            quantise_w(1)
-            quantise_agg(1)
-            linear_bn_relu(0, 1)
-            turn_back_and_store(0, 0)
-            linear_bn_relu(1, 0)
-            turn_back_and_store(0, 1)
-            linear_bn_relu(1, 1)
-            turn_back_and_store(1, 0)
-            turn_back_and_store(1, 1)
+            for tb in (4, 5):
+                for g in range(G):
+                    aggregate(g, tb)
+            for g in range(G):
+                aggregate(g, 6)
+            regroup_w(1, 0)
+            quantise_w(0, 0)
+            quantise_w(1, 0)
+            for g in range(G):
+                quantise_agg(g, 0, 4)
+            linear_bn_relu(0, 4, 0, 4)
+            regroup_w(0, 1)
+            regroup_w(1, 1)
+            quantise_w(0, 1)
+            quantise_w(1, 1)
+            for g in range(G):
+                aggregate(g, 7)
+            turn_back_vector(0, 2, 0)
+            store_vector(0, 2, 0)
+            linear_bn_relu(0, 4, 4, 8)
+            for g in range(G):
+                quantise_agg(g, 4)
+            turn_back_vector(2, 2, 0)
+            store_vector(2, 2, 0)
+            for g in range(G):
+                quantise_agg(g, 6)
+            turn_back_vector(0, 2, 1)
+            store_vector(0, 2, 1)
+            linear_bn_relu(4, 2, 0, 4)
+            turn_back_vector(2, 2, 1)
+            store_vector(2, 2, 1)
+            linear_bn_relu(4, 2, 4, 8)
+            turn_back_vector(4, 2, 0)
+            store_vector(4, 2, 0)
+            linear_bn_relu(6, 2, 0, 8)
+            turn_back_vector(4, 2, 1)
+            store_vector(4, 2, 1)
+            turn_back_tensor(6)
+            turn_back_tensor(7)

@@ -203,15 +203,23 @@ def tile_bipartitegcnstack_pa_kernel(
             par_ps = psum.tile([P, P], BF16, tag="bank")
             nc.tensor.transpose(par_ps[:], par_rows[:], ident_bf[:])
             nc.scalar.copy(out=par[:].rearrange("p v hb -> p (v hb)"), in_=par_ps[:, 0 : len(vectors) * HB])
-            nc.gpsimd.tensor_scalar_add(out=std[:], in0=var_c, scalar1=EPS_BN)
+
+        def fold_0():
+            nc.vector.tensor_scalar_add(out=std[:], in0=var_c, scalar1=EPS_BN)
             nc.scalar.activation(out=std[:], in_=std[:], func=ACT.Sqrt)
 
-        def scale_and_shift():
+        def fold_1():
             nc.vector.reciprocal(out=scale_c[:], in_=std[:])
-            nc.gpsimd.tensor_mul(out=scale_c[:], in0=scale_c[:], in1=gamma_c)
-            nc.gpsimd.tensor_sub(out=shift_c[:], in0=bias_c, in1=mean_c)
-            nc.gpsimd.tensor_mul(out=shift_c[:], in0=shift_c[:], in1=scale_c[:])
-            nc.gpsimd.tensor_add(out=shift_c[:], in0=shift_c[:], in1=beta_c)
+            nc.vector.tensor_sub(out=shift_c[:], in0=bias_c, in1=mean_c)
+
+        def fold_2():
+            nc.vector.tensor_mul(out=scale_c[:], in0=scale_c[:], in1=gamma_c)
+
+        def fold_3():
+            nc.vector.tensor_mul(out=shift_c[:], in0=shift_c[:], in1=scale_c[:])
+
+        def fold_4():
+            nc.vector.tensor_add(out=shift_c[:], in0=shift_c[:], in1=beta_c)
 
         def aggregate(g, tb, on_vector=False):
             t_cols = slice(tb * P, (tb + 1) * P)
@@ -348,17 +356,21 @@ def tile_bipartitegcnstack_pa_kernel(
             regroup_w(0, 0)
             quantise_a(4)
             quantise_a(6)
-            scale_and_shift()
+            fold_0()
             for tb in (4, 5):
                 for g in range(G):
                     aggregate(g, tb)
             for g in range(G):
                 aggregate(g, 6)
             regroup_w(1, 0)
+            fold_1()
             quantise_w(0, 0)
+            fold_2()
             quantise_w(1, 0)
-            for g in range(G):
-                quantise_agg(g, 0, 4)
+            fold_3()
+            quantise_agg(0, 0, 4)
+            fold_4()
+            quantise_agg(1, 0, 4)
             linear_bn_relu(0, 4, 0, 4)
             regroup_w(0, 1)
             regroup_w(1, 1)

@@ -27,7 +27,7 @@ G = DS // K_PASS
 HALF = 512
 HQ = HB // 2
 PAIR = 2
-V_TB = 6
+V_UNITS = ((0, 0), (2, 0), (0, 1), (2, 1))
 JB = P // BLK
 
 FLOPS = 2 * NT * NS * DS + 2 * NT * DS * DH
@@ -62,10 +62,10 @@ def tile_bipartitegcnstack_pa_kernel(
         agg_codes = keep.tile([P, G, NT], U32, align_bytes=64)
         agg_scales = keep.tile([P, G, NT], U8, align_bytes=64)
 
-        y_t = keep.tile([P, 2, V_TB * JB, HQ, BLK], F32, align_bytes=64)
-        y_v = keep.tile([P, 2, V_TB * JB, HQ, BLK], F32, align_bytes=64)
-        y_p = keep.tile([P, HB, (TB - V_TB) * P], F32)
-        y_o = keep.tile([P, TB - V_TB, QUADS, HB, BLK], F32)
+        y_t = keep.tile([P, len(V_UNITS), PAIR * JB, HQ, BLK], F32, align_bytes=64)
+        y_v = keep.tile([P, len(V_UNITS), PAIR * JB, HQ, BLK], F32, align_bytes=64)
+        y_p = keep.tile([P, HB, NT], F32)
+        y_o = keep.tile([P, TB, QUADS, HB, BLK], F32)
 
         vectors = [b0, bn_gamma, bn_beta, bn_mean, bn_var]
         par_rows = keep.tile([P, P], BF16)
@@ -87,7 +87,6 @@ def tile_bipartitegcnstack_pa_kernel(
 
         def load_everything():
             nc.vector.memset(par_rows[:], 0.0)
-
             def load_a(t0, t1):
                 nc.sync.dma_start(out=a_raw[:, t0:t1, :], in_=a_view[:, t0:t1, :])
 
@@ -115,8 +114,8 @@ def tile_bipartitegcnstack_pa_kernel(
         def constants():
             nc.vector.memset(warm[:], 1.0)
             nc.scalar.activation(out=warm[:], in_=warm[:], func=ACT.Sqrt)
-            make_identity(nc, ident_f32[:])
             make_identity(nc, ident_bf[:])
+            make_identity(nc, ident_f32[:])
 
         def row_sum_vector(tb):
             unused = scratch.tile([P, NS], BF16)
@@ -181,9 +180,9 @@ def tile_bipartitegcnstack_pa_kernel(
                 in_=h_grouped[:, cols, :].rearrange("p c j -> p (c j)"),
             )
 
-        def regroup_w(g, half):
+        def regroup_w(g, half, copy=nc.vector.tensor_copy):
             for hb in range(half * HB // 2, (half + 1) * HB // 2):
-                nc.vector.tensor_copy(
+                copy(
                     out=w_grouped[:, g, hb, :, :].rearrange("p (i c k) j -> p i c j k", i=QUADS, k=4),
                     in_=w_raw[:, g * PACK : (g + 1) * PACK, :].rearrange(
                         "p j (i hb c k) -> p hb i c j k", i=QUADS, hb=HB, k=4
@@ -202,7 +201,7 @@ def tile_bipartitegcnstack_pa_kernel(
         def turn_vectors():
             par_ps = psum.tile([P, P], BF16, tag="bank")
             nc.tensor.transpose(par_ps[:], par_rows[:], ident_bf[:])
-            nc.scalar.copy(out=par[:].rearrange("p v hb -> p (v hb)"), in_=par_ps[:, 0 : len(vectors) * HB])
+            nc.vector.tensor_copy(out=par[:].rearrange("p v hb -> p (v hb)"), in_=par_ps[:, 0 : len(vectors) * HB])
 
         def fold_0():
             nc.vector.tensor_scalar_add(out=std[:], in0=var_c, scalar1=EPS_BN)
@@ -264,11 +263,12 @@ def tile_bipartitegcnstack_pa_kernel(
                         start=(g == 0),
                         stop=(g == G - 1),
                     )
-                if tb0 < V_TB:
-                    dst = y_t[:, hb // HQ, tb0 * JB : (tb0 + n) * JB, hb % HQ, :]
-                    src = acc[:].rearrange("p (j a) -> p j a", a=BLK)
+                if (tb0, hb // HQ) in V_UNITS:
+                    unit = V_UNITS.index((tb0, hb // HQ))
+                    dst = y_t[:, unit : unit + n // PAIR, :, hb % HQ, :]
+                    src = acc[:].rearrange("p (u j a) -> p u j a", j=PAIR * JB, a=BLK)
                 else:
-                    dst = y_p[:, hb, (tb0 - V_TB) * P : (tb0 - V_TB + n) * P]
+                    dst = y_p[:, hb, t_cols]
                     src = acc[:]
                 nc.scalar.activation(
                     out=dst,
@@ -278,38 +278,37 @@ def tile_bipartitegcnstack_pa_kernel(
                     scale=scale_c[:, hb : hb + 1],
                 )
 
-        def turn_back_vector(tb, n, half):
-            js = slice(tb * JB, (tb + n) * JB)
+        def turn_back_vector(tb0, half):
+            unit = V_UNITS.index((tb0, half))
             nc.vector.transpose(
-                y_v[:, half, js, :, :].rearrange("p j hb b -> p (j hb b)"),
-                y_t[:, half, js, :, :].rearrange("p j hb a -> p (j hb a)"),
+                y_v[:, unit].rearrange("p j hb b -> p (j hb b)"),
+                y_t[:, unit].rearrange("p j hb a -> p (j hb a)"),
             )
 
-        def store_vector(tb0, n, half):
-            js = slice(tb0 * JB, (tb0 + n) * JB)
-            rows = out[tb0 * P : (tb0 + n) * P, :].rearrange("(j a) (i x c) -> i x a j c", a=BLK, i=QUADS, x=2)
+        def store_vector(tb0, half):
+            unit = V_UNITS.index((tb0, half))
+            rows = out[tb0 * P : (tb0 + PAIR) * P, :].rearrange("(j a) (i x c) -> i x a j c", a=BLK, i=QUADS, x=2)
             for i in (0, 2, 1, 3):
                 nc.sync.dma_start(
                     out=rows[i, half],
-                    in_=y_v[i * BLK : (i + 1) * BLK, half, js, :, :].rearrange("p j hb b -> p j (hb b)"),
+                    in_=y_v[i * BLK : (i + 1) * BLK, unit].rearrange("p j hb b -> p j (hb b)"),
                 )
 
-        def turn_back_tensor(tb):
-            x = tb - V_TB
-            for half in range(2):
-                turned = psum.tile([P, HB // 2, P], F32, tag="bank")
-                for q in range(HB // 2):
-                    nc.tensor.transpose(
-                        turned[:, q, :], y_p[:, half * HB // 2 + q, x * P : (x + 1) * P], ident_f32[:]
-                    )
-                dst = y_o[:, x, :, half * HB // 2 : (half + 1) * HB // 2, :].rearrange("p i q b -> p q i b")
-                src = turned[:].rearrange("p q (i b) -> p q i b", b=BLK)
-                if half == 0:
-                    nc.scalar.copy(out=dst, in_=src)
-                else:
-                    nc.vector.tensor_copy(out=dst, in_=src)
+        def turn_back_tensor(tb, half, on_scalar=False):
+            turned = psum.tile([P, HQ, P], F32, tag="bank")
+            for q in range(HQ):
+                nc.tensor.transpose(turned[:, q, :], y_p[:, half * HQ + q, tb * P : (tb + 1) * P], ident_f32[:])
+            dst = y_o[:, tb, :, half * HQ : (half + 1) * HQ, :].rearrange("p i q b -> p q i b")
+            src = turned[:].rearrange("p q (i b) -> p q i b", b=BLK)
+            if on_scalar:
+                nc.scalar.copy(out=dst, in_=src)
+            else:
+                nc.vector.tensor_copy(out=dst, in_=src)
+
+        def store_tensor(tb, half):
             nc.sync.dma_start(
-                out=out[tb * P : (tb + 1) * P, :], in_=y_o[:, x].rearrange("p i hb b -> p (i hb b)")
+                out=out[tb * P : (tb + 1) * P, :].rearrange("p (i x c) -> x p i c", i=QUADS, x=2)[half],
+                in_=y_o[:, tb, :, half * HQ : (half + 1) * HQ, :].rearrange("p i hb b -> p i (hb b)"),
             )
 
         with tc.manual_schedule():
@@ -317,86 +316,92 @@ def tile_bipartitegcnstack_pa_kernel(
             constants()
             row_sum_vector(0)
             row_sum_scalar(1)
-            row_sum_scalar(3)
             row_sum_vector(2)
+            row_sum_scalar(3)
             clamp(0, 2)
             invert(0, 2)
             normalise(0)
             normalise(1)
             transpose_a(0)
+            row_sum_scalar(4)
+            row_sum_scalar(5)
             clamp(2, 4)
             invert(2, 4)
             normalise(2)
             normalise(3)
             transpose_a(2)
-            regroup_h(0)
-            row_sum_scalar(5)
             row_sum_scalar(6)
+            row_sum_scalar(7)
+            regroup_h(0)
             quantise_a(0)
             quantise_h(0)
             quantise_a(2)
             for tb in range(4):
                 aggregate(0, tb)
             regroup_h(1)
-            row_sum_vector(4)
             quantise_h(1)
-            row_sum_vector(7)
+            turn_vectors()
+            fold_0()
+            for tb in range(4):
+                aggregate(1, tb)
+            regroup_w(0, 0)
             clamp(4, 8)
-
+            fold_1()
             invert(4, 8)
             for tb in range(4, TB):
                 normalise(tb)
-            for tb in range(2):
-                aggregate(1, tb)
             transpose_a(4)
             transpose_a(6)
-            turn_vectors()
-            for tb in range(2, 4):
-                aggregate(1, tb)
-            regroup_w(0, 0)
-            quantise_a(4)
-            quantise_a(6)
-            fold_0()
-            for tb in (4, 5):
-                for g in range(G):
-                    aggregate(g, tb)
-            for g in range(G):
-                aggregate(g, 6)
-            regroup_w(1, 0)
-            fold_1()
+            regroup_w(0, 1, nc.scalar.copy)
             quantise_w(0, 0)
+            regroup_w(1, 0)
             fold_2()
-            quantise_w(1, 0)
-            fold_3()
             quantise_agg(0, 0, 4)
+            fold_3()
+            quantise_w(1, 0)
             fold_4()
             quantise_agg(1, 0, 4)
             linear_bn_relu(0, 4, 0, 4)
-            regroup_w(0, 1)
             regroup_w(1, 1)
+            quantise_a(4)
+            quantise_a(6)
+            for tb in (4, 5):
+                for g in range(G):
+                    aggregate(g, tb)
             quantise_w(0, 1)
             quantise_w(1, 1)
-            for g in range(G):
-                aggregate(g, 7)
-            turn_back_vector(0, 2, 0)
-            store_vector(0, 2, 0)
+            turn_back_vector(0, 0)
+            store_vector(0, 0)
             linear_bn_relu(0, 4, 4, 8)
+            turn_back_vector(2, 0)
+            store_vector(2, 0)
             for g in range(G):
                 quantise_agg(g, 4)
-            turn_back_vector(2, 2, 0)
-            store_vector(2, 2, 0)
+            for g in range(G):
+                aggregate(g, 6)
+            for g in range(G):
+                aggregate(g, 7, True)
+            turn_back_vector(0, 1)
+            store_vector(0, 1)
+            linear_bn_relu(4, 2, 0, 8)
             for g in range(G):
                 quantise_agg(g, 6)
-            turn_back_vector(0, 2, 1)
-            store_vector(0, 2, 1)
-            linear_bn_relu(4, 2, 0, 4)
-            turn_back_vector(2, 2, 1)
-            store_vector(2, 2, 1)
-            linear_bn_relu(4, 2, 4, 8)
-            turn_back_vector(4, 2, 0)
-            store_vector(4, 2, 0)
+            turn_back_vector(2, 1)
+            store_vector(2, 1)
             linear_bn_relu(6, 2, 0, 8)
-            turn_back_vector(4, 2, 1)
-            store_vector(4, 2, 1)
-            turn_back_tensor(6)
-            turn_back_tensor(7)
+            turn_back_tensor(4, 0)
+            store_tensor(4, 0)
+            turn_back_tensor(5, 0)
+            store_tensor(5, 0)
+            turn_back_tensor(4, 1)
+            store_tensor(4, 1)
+            turn_back_tensor(5, 1)
+            store_tensor(5, 1)
+            turn_back_tensor(6, 0)
+            store_tensor(6, 0)
+            turn_back_tensor(7, 0, True)
+            store_tensor(7, 0)
+            turn_back_tensor(6, 1)
+            store_tensor(6, 1)
+            turn_back_tensor(7, 1, True)
+            store_tensor(7, 1)

@@ -25,6 +25,8 @@ TB = NT // P
 HB = DH // P
 G = DS // K_PASS
 HALF = 512
+CHUNK_TB = 4
+CHUNK = CHUNK_TB * P
 HQ = HB // 2
 PAIR = 2
 V_UNITS = ((0, 0), (2, 0), (0, 1), (2, 1))
@@ -81,35 +83,25 @@ def tile_bipartitegcnstack_pa_kernel(
         ident_bf = keep.tile([P, P], BF16)
         ident_f32 = keep.tile([P, P], F32)
 
-        a_view = A.rearrange("(tb p) s -> p tb s", p=P)
-        h_view = H_source.rearrange("(p j) d -> p j d", j=PACK)
+        a_first = A[0:CHUNK, :].rearrange("(tb p) s -> p tb s", p=P)
+        a_second = A[CHUNK:NT, :].rearrange("(p x) s -> p x s", p=P)
+        out_second = out[CHUNK:NT, :].rearrange("(p x) h -> p x h", p=P)
         w_view = W0.rearrange("(gj p) h -> p gj h", p=P)
 
         def load_everything():
             nc.vector.memset(par_rows[:], 0.0)
-            def load_a(t0, t1):
-                nc.sync.dma_start(out=a_raw[:, t0:t1, :], in_=a_view[:, t0:t1, :])
-
-            def load_h(half):
-                cols = slice(half * HALF, (half + 1) * HALF)
-                nc.sync.dma_start(out=h_raw[:, :, cols], in_=h_view[:, :, cols])
-
-            def load_w(g):
-                js = slice(g * PACK, (g + 1) * PACK)
-                nc.sync.dma_start(out=w_raw[:, js, :], in_=w_view[:, js, :])
-
-            load_a(0, 2)
-            load_a(2, 4)
-            load_h(0)
-            load_a(4, 8)
-            load_h(1)
-            load_w(0)
+            nc.sync.dma_start(out=a_raw[:, 0:PAIR, :], in_=a_first[:, 0:PAIR, :])
             for v, vector in enumerate(vectors):
                 nc.sync.dma_start(
                     out=par_rows[v * HB : (v + 1) * HB, :].rearrange("hb (i b) -> hb i b", b=BLK),
                     in_=vector.rearrange("(i hb b) -> hb i b", hb=HB, b=BLK),
                 )
-            load_w(1)
+            nc.sync.dma_start(out=a_raw[:, PAIR:CHUNK_TB, :], in_=a_first[:, PAIR:CHUNK_TB, :])
+            nc.sync.dma_start(out=h_raw[:], in_=H_source.rearrange("(p j) d -> p j d", j=PACK))
+            nc.sync.dma_start(out=a_raw[:, CHUNK_TB:TB, :], in_=a_second)
+            for g in range(G):
+                js = slice(g * PACK, (g + 1) * PACK)
+                nc.sync.dma_start(out=w_raw[:, js, :], in_=w_view[:, js, :])
 
         def constants():
             nc.vector.memset(warm[:], 1.0)
@@ -248,6 +240,12 @@ def tile_bipartitegcnstack_pa_kernel(
                 in_=agg_grouped[:, g, tb0 : tb0 + n, :, :].rearrange("p tb t j -> p (tb t j)"),
             )
 
+        def warm_up(passes):
+            wide = w_grouped[:, 1, 0, :, :].rearrange("p m j -> p (m j)")
+            unread = psum.tile([P, HALF], F32, tag="bank")
+            for step in range(passes):
+                nc.tensor.matmul(unread[:], lhsT=wide[:, 0:P], rhs=wide, start=True, stop=True)
+
         def linear_bn_relu(tb0, n, hb0, hb1):
             t_cols = slice(tb0 * P, (tb0 + n) * P)
             for hb in range(hb0, hb1):
@@ -305,10 +303,9 @@ def tile_bipartitegcnstack_pa_kernel(
             else:
                 nc.vector.tensor_copy(out=dst, in_=src)
 
-        def store_tensor(tb, half):
+        def store_tensor(tb):
             nc.sync.dma_start(
-                out=out[tb * P : (tb + 1) * P, :].rearrange("p (i x c) -> x p i c", i=QUADS, x=2)[half],
-                in_=y_o[:, tb, :, half * HQ : (half + 1) * HQ, :].rearrange("p i hb b -> p i (hb b)"),
+                out=out_second[:, tb - CHUNK_TB, :], in_=y_o[:, tb, :, :, :].rearrange("p i hb b -> p (i hb b)")
             )
 
         with tc.manual_schedule():
@@ -316,22 +313,26 @@ def tile_bipartitegcnstack_pa_kernel(
             constants()
             row_sum_vector(0)
             row_sum_scalar(1)
+            turn_vectors()
+            fold_0()
             row_sum_vector(2)
             row_sum_scalar(3)
             clamp(0, 2)
+            fold_1()
             invert(0, 2)
+            fold_2()
             normalise(0)
             normalise(1)
             transpose_a(0)
-            row_sum_scalar(4)
-            row_sum_scalar(5)
             clamp(2, 4)
+            fold_3()
             invert(2, 4)
+            fold_4()
             normalise(2)
             normalise(3)
             transpose_a(2)
-            row_sum_scalar(6)
-            row_sum_scalar(7)
+            for tb in range(4, TB):
+                row_sum_scalar(tb)
             regroup_h(0)
             quantise_a(0)
             quantise_h(0)
@@ -340,28 +341,23 @@ def tile_bipartitegcnstack_pa_kernel(
                 aggregate(0, tb)
             regroup_h(1)
             quantise_h(1)
-            turn_vectors()
-            fold_0()
             for tb in range(4):
                 aggregate(1, tb)
             regroup_w(0, 0)
             clamp(4, 8)
-            fold_1()
             invert(4, 8)
             for tb in range(4, TB):
                 normalise(tb)
             transpose_a(4)
             transpose_a(6)
-            regroup_w(0, 1, nc.scalar.copy)
             quantise_w(0, 0)
             regroup_w(1, 0)
-            fold_2()
+            warm_up(4)
             quantise_agg(0, 0, 4)
-            fold_3()
             quantise_w(1, 0)
-            fold_4()
             quantise_agg(1, 0, 4)
             linear_bn_relu(0, 4, 0, 4)
+            regroup_w(0, 1)
             regroup_w(1, 1)
             quantise_a(4)
             quantise_a(6)
@@ -377,8 +373,8 @@ def tile_bipartitegcnstack_pa_kernel(
             store_vector(2, 0)
             for g in range(G):
                 quantise_agg(g, 4)
-            for g in range(G):
-                aggregate(g, 6)
+            aggregate(0, 6, True)
+            aggregate(1, 6)
             for g in range(G):
                 aggregate(g, 7, True)
             turn_back_vector(0, 1)
@@ -388,20 +384,17 @@ def tile_bipartitegcnstack_pa_kernel(
                 quantise_agg(g, 6)
             turn_back_vector(2, 1)
             store_vector(2, 1)
-            linear_bn_relu(6, 2, 0, 8)
+            linear_bn_relu(6, 2, 0, 4)
             turn_back_tensor(4, 0)
-            store_tensor(4, 0)
             turn_back_tensor(5, 0)
-            store_tensor(5, 0)
+            linear_bn_relu(6, 2, 4, 8)
             turn_back_tensor(4, 1)
-            store_tensor(4, 1)
-            turn_back_tensor(5, 1)
-            store_tensor(5, 1)
+            store_tensor(4)
+            turn_back_tensor(5, 1, True)
+            store_tensor(5)
             turn_back_tensor(6, 0)
-            store_tensor(6, 0)
             turn_back_tensor(7, 0, True)
-            store_tensor(7, 0)
             turn_back_tensor(6, 1)
-            store_tensor(6, 1)
+            store_tensor(6)
             turn_back_tensor(7, 1, True)
-            store_tensor(7, 1)
+            store_tensor(7)

@@ -357,10 +357,10 @@ def tile_bipartitegcnstack_pa_kernel(
             quantise_w(1, 0)
             quantise_agg(1, 0, 4)
             linear_bn_relu(0, 4, 0, 4)
-            regroup_w(0, 1)
-            regroup_w(1, 1)
             quantise_a(4)
             quantise_a(6)
+            regroup_w(0, 1)
+            regroup_w(1, 1)
             for tb in (4, 5):
                 for g in range(G):
                     aggregate(g, tb)
@@ -373,10 +373,10 @@ def tile_bipartitegcnstack_pa_kernel(
             store_vector(2, 0)
             for g in range(G):
                 quantise_agg(g, 4)
-            aggregate(0, 6, True)
-            aggregate(1, 6)
+            aggregate(0, 7, True)
+            aggregate(1, 7, True)
             for g in range(G):
-                aggregate(g, 7, True)
+                aggregate(g, 6)
             turn_back_vector(0, 1)
             store_vector(0, 1)
             linear_bn_relu(4, 2, 0, 8)
@@ -387,11 +387,11 @@ def tile_bipartitegcnstack_pa_kernel(
             linear_bn_relu(6, 2, 0, 4)
             turn_back_tensor(4, 0)
             turn_back_tensor(5, 0)
-            linear_bn_relu(6, 2, 4, 8)
             turn_back_tensor(4, 1)
             store_tensor(4)
             turn_back_tensor(5, 1, True)
             store_tensor(5)
+            linear_bn_relu(6, 2, 4, 8)
             turn_back_tensor(6, 0)
             turn_back_tensor(7, 0, True)
             turn_back_tensor(6, 1)

@@ -172,8 +172,8 @@ def tile_bipartitegcnstack_pa_kernel(
                 in_=h_grouped[:, cols, :].rearrange("p c j -> p (c j)"),
             )
 
-        def regroup_w(g, half, copy=nc.vector.tensor_copy):
-            for hb in range(half * HB // 2, (half + 1) * HB // 2):
+        def regroup_w(g, hb0, hb1, copy=nc.vector.tensor_copy):
+            for hb in range(hb0, hb1):
                 copy(
                     out=w_grouped[:, g, hb, :, :].rearrange("p (i c k) j -> p i c j k", i=QUADS, k=4),
                     in_=w_raw[:, g * PACK : (g + 1) * PACK, :].rearrange(
@@ -341,17 +341,20 @@ def tile_bipartitegcnstack_pa_kernel(
                 aggregate(0, tb)
             regroup_h(1)
             quantise_h(1)
-            for tb in range(4):
+            for tb in range(2):
                 aggregate(1, tb)
-            regroup_w(0, 0)
+            for tb in range(2, 4):
+                aggregate(1, tb)
+            regroup_w(0, 0, 4)
             clamp(4, 8)
             invert(4, 8)
             for tb in range(4, TB):
                 normalise(tb)
             transpose_a(4)
             transpose_a(6)
+            regroup_w(0, 7, 8, nc.scalar.copy)
             quantise_w(0, 0)
-            regroup_w(1, 0)
+            regroup_w(1, 0, 4)
             warm_up(4)
             quantise_agg(0, 0, 4)
             quantise_w(1, 0)
@@ -359,8 +362,8 @@ def tile_bipartitegcnstack_pa_kernel(
             linear_bn_relu(0, 4, 0, 4)
             quantise_a(4)
             quantise_a(6)
-            regroup_w(0, 1)
-            regroup_w(1, 1)
+            regroup_w(0, 4, 7)
+            regroup_w(1, 4, 8)
             for tb in (4, 5):
                 for g in range(G):
                     aggregate(g, tb)
@@ -386,15 +389,15 @@ def tile_bipartitegcnstack_pa_kernel(
             store_vector(2, 1)
             linear_bn_relu(6, 2, 0, 4)
             turn_back_tensor(4, 0)
-            turn_back_tensor(5, 0)
-            turn_back_tensor(4, 1)
+            turn_back_tensor(4, 1, True)
             store_tensor(4)
-            turn_back_tensor(5, 1, True)
+            turn_back_tensor(5, 0)
+            turn_back_tensor(5, 1)
             store_tensor(5)
             linear_bn_relu(6, 2, 4, 8)
             turn_back_tensor(6, 0)
-            turn_back_tensor(7, 0, True)
-            turn_back_tensor(6, 1)
+            turn_back_tensor(6, 1, True)
             store_tensor(6)
+            turn_back_tensor(7, 0)
             turn_back_tensor(7, 1, True)
             store_tensor(7)

@@ -335,19 +335,21 @@ def tile_bipartitegcnstack_pa_kernel(
                 row_sum_scalar(tb)
             regroup_h(0)
             quantise_a(0)
+            regroup_h(1)
             quantise_h(0)
             quantise_a(2)
             for tb in range(4):
                 aggregate(0, tb)
-            regroup_h(1)
             quantise_h(1)
             for tb in range(2):
                 aggregate(1, tb)
             for tb in range(2, 4):
                 aggregate(1, tb)
-            regroup_w(0, 0, 4)
+            regroup_w(0, 0, 1)
             clamp(4, 8)
+            regroup_w(0, 1, 3)
             invert(4, 8)
+            regroup_w(0, 3, 4)
             for tb in range(4, TB):
                 normalise(tb)
             transpose_a(4)

from contextlib import ExitStack

import concourse.mybir as mybir
from concourse.masks import make_identity

BF16 = mybir.dt.bfloat16
F32 = mybir.dt.float32
U32 = mybir.dt.uint32
U8 = mybir.dt.uint8
FP8X4 = mybir.dt.float8_e4m3fn_x4
ACT = mybir.ActivationFunctionType
ALU = mybir.AluOpType

P = 128
PACK = 4
K_PASS = P * PACK
BLK = 32
QUADS = P // BLK

NS, NT, DS, DH = 512, 1024, 1024, 1024
EPS_ROW = 1e-8
EPS_BN = 1e-5

TB = NT // P
HB = DH // P
G = DS // K_PASS
HALF = 512
CHUNK_TB = 4
CHUNK = CHUNK_TB * P
HQ = HB // 2
PAIR = 2
V_UNITS = ((0, 0), (2, 0), (0, 1), (2, 1))
JB = P // BLK

FLOPS = 2 * NT * NS * DS + 2 * NT * DS * DH


def tile_bipartitegcnstack_pa_kernel(
    tc, H_source, A, W0, b0, bn_gamma, bn_beta, bn_mean, bn_var, out
):
    nc = tc.nc
    with ExitStack() as ctx:
        keep = ctx.enter_context(tc.tile_pool(name="keep", bufs=1))
        scratch = ctx.enter_context(tc.tile_pool(name="scratch", bufs=2))
        psum = ctx.enter_context(tc.psum_pool(name="psum", bufs=8))

        a_raw = keep.tile([P, TB, NS], BF16)
        a_norm = keep.tile([P, TB, NS], BF16)
        a_grouped = keep.tile([P, TB, P, PACK], BF16, align_bytes=64)
        a_codes = keep.tile([P, NT], U32, align_bytes=64)
        a_scales = keep.tile([P, NT], U8, align_bytes=64)

        h_raw = keep.tile([P, PACK, DS], BF16)
        h_grouped = keep.tile([P, DS, PACK], BF16, align_bytes=64)
        h_codes = keep.tile([P, DS], U32, align_bytes=64)
        h_scales = keep.tile([P, DS], U8, align_bytes=64)

        w_raw = keep.tile([P, G * PACK, DH], BF16)
        w_grouped = keep.tile([P, G, HB, P, PACK], BF16, align_bytes=64)
        w_codes = keep.tile([P, G, DH], U32, align_bytes=64)
        w_scales = keep.tile([P, G, DH], U8, align_bytes=64)

        agg_grouped = keep.tile([P, G, TB, P, PACK], BF16, align_bytes=64)
        agg_codes = keep.tile([P, G, NT], U32, align_bytes=64)
        agg_scales = keep.tile([P, G, NT], U8, align_bytes=64)

        y_t = keep.tile([P, len(V_UNITS), PAIR * JB, HQ, BLK], F32, align_bytes=64)
        y_v = keep.tile([P, len(V_UNITS), PAIR * JB, HQ, BLK], F32, align_bytes=64)
        y_p = keep.tile([P, HB, NT], F32)
        y_o = keep.tile([P, TB, QUADS, HB, BLK], F32)

        vectors = [b0, bn_gamma, bn_beta, bn_mean, bn_var]
        par_rows = keep.tile([P, P], BF16)
        par = keep.tile([P, len(vectors), HB], F32)
        bias_c, gamma_c, beta_c, mean_c, var_c = [par[:, v, :] for v in range(len(vectors))]
        std = keep.tile([P, HB], F32)
        scale_c = keep.tile([P, HB], F32)
        shift_c = keep.tile([P, HB], F32)

        row_sum = keep.tile([P, TB], F32)
        row_inv = keep.tile([P, TB], F32)
        warm = keep.tile([P, 1], F32)
        ident_bf = keep.tile([P, P], BF16)
        ident_f32 = keep.tile([P, P], F32)

        a_first = A[0:CHUNK, :].rearrange("(tb p) s -> p tb s", p=P)
        a_second = A[CHUNK:NT, :].rearrange("(p x) s -> p x s", p=P)
        out_second = out[CHUNK:NT, :].rearrange("(p x) h -> p x h", p=P)
        w_view = W0.rearrange("(gj p) h -> p gj h", p=P)

        def load_everything():
            nc.vector.memset(par_rows[:], 0.0)
            nc.sync.dma_start(out=a_raw[:, 0:PAIR, :], in_=a_first[:, 0:PAIR, :])
            for v, vector in enumerate(vectors):
                nc.sync.dma_start(
                    out=par_rows[v * HB : (v + 1) * HB, :].rearrange("hb (i b) -> hb i b", b=BLK),
                    in_=vector.rearrange("(i hb b) -> hb i b", hb=HB, b=BLK),
                )
            nc.sync.dma_start(out=a_raw[:, PAIR:CHUNK_TB, :], in_=a_first[:, PAIR:CHUNK_TB, :])
            nc.sync.dma_start(out=h_raw[:], in_=H_source.rearrange("(p j) d -> p j d", j=PACK))
            nc.sync.dma_start(out=a_raw[:, CHUNK_TB:TB, :], in_=a_second)
            for g in range(G):
                js = slice(g * PACK, (g + 1) * PACK)
                nc.sync.dma_start(out=w_raw[:, js, :], in_=w_view[:, js, :])

        def constants():
            nc.vector.memset(warm[:], 1.0)
            nc.scalar.activation(out=warm[:], in_=warm[:], func=ACT.Sqrt)
            make_identity(nc, ident_bf[:])
            make_identity(nc, ident_f32[:])

        def row_sum_vector(tb):
            unused = scratch.tile([P, NS], BF16)
            nc.vector.tensor_scalar(
                out=unused[:],
                in0=a_raw[:, tb, :],
                scalar1=1.0,
                scalar2=None,
                op0=ALU.mult,
                op1=ALU.add,
                accum_out=row_sum[:, tb : tb + 1],
            )

        def row_sum_scalar(tb):
            unused_s = scratch.tile([P, NS], BF16)
            nc.scalar.activation(
                out=unused_s[:], in_=a_raw[:, tb, :], func=ACT.Copy, accum_out=row_sum[:, tb : tb + 1]
            )

        def clamp(t0, t1):
            nc.vector.tensor_scalar_max(out=row_inv[:, t0:t1], in0=row_sum[:, t0:t1], scalar1=EPS_ROW)

        def invert(t0, t1):
            nc.vector.reciprocal(out=row_inv[:, t0:t1], in_=row_inv[:, t0:t1])

        def normalise(tb):
            nc.vector.tensor_scalar_mul(
                out=a_norm[:, tb, :], in0=a_raw[:, tb, :], scalar1=row_inv[:, tb : tb + 1]
            )

        def transpose_a(tb0):
            turned = psum.tile([P, PAIR, 2, P], F32, tag="bank")
            for b in range(PAIR):
                words = a_norm[:, tb0 + b, :].bitcast(F32)
                for u in range(2):
                    nc.tensor.transpose(turned[:, b, u, :], words[:, u::2], ident_f32[:])
            nc.scalar.copy(
                out=a_grouped[:, tb0 : tb0 + PAIR, :, :].bitcast(F32),
                in_=turned[:].rearrange("p b u t -> p b t u"),
            )

        def quantise_a(tb0):
            cols = slice(tb0 * P, (tb0 + PAIR) * P)
            nc.vector.quantize_mx(
                out=a_codes[:, cols].bitcast(FP8X4),
                scales=a_scales[:, cols],
                in_=a_grouped[:, tb0 : tb0 + PAIR, :, :].rearrange("p tb t j -> p (tb t j)"),
            )

        def regroup_h(half):
            cols = slice(half * HALF, (half + 1) * HALF)
            nc.vector.tensor_copy(
                out=h_grouped[:, cols, :].rearrange("p (c i) j -> p c j i", i=4),
                in_=h_raw[:, :, cols].rearrange("p j (c i) -> p c j i", i=4),
            )

        def quantise_h(half):
            cols = slice(half * HALF, (half + 1) * HALF)
            nc.vector.quantize_mx(
                out=h_codes[:, cols].bitcast(FP8X4),
                scales=h_scales[:, cols],
                in_=h_grouped[:, cols, :].rearrange("p c j -> p (c j)"),
            )

        def regroup_w(g, hb0, hb1, copy=nc.vector.tensor_copy):
            for hb in range(hb0, hb1):
                copy(
                    out=w_grouped[:, g, hb, :, :].rearrange("p (i c k) j -> p i c j k", i=QUADS, k=4),
                    in_=w_raw[:, g * PACK : (g + 1) * PACK, :].rearrange(
                        "p j (i hb c k) -> p hb i c j k", i=QUADS, hb=HB, k=4
                    )[:, hb],
                )

        def quantise_w(g, half):
            cols = slice(half * HALF, (half + 1) * HALF)
            hbs = slice(half * HB // 2, (half + 1) * HB // 2)
            nc.vector.quantize_mx(
                out=w_codes[:, g, cols].bitcast(FP8X4),
                scales=w_scales[:, g, cols],
                in_=w_grouped[:, g, hbs, :, :].rearrange("p hb m j -> p (hb m j)"),
            )

        def turn_vectors():
            par_ps = psum.tile([P, P], BF16, tag="bank")
            nc.tensor.transpose(par_ps[:], par_rows[:], ident_bf[:])
            nc.vector.tensor_copy(out=par[:].rearrange("p v hb -> p (v hb)"), in_=par_ps[:, 0 : len(vectors) * HB])

        def fold_0():
            nc.vector.tensor_scalar_add(out=std[:], in0=var_c, scalar1=EPS_BN)
            nc.scalar.activation(out=std[:], in_=std[:], func=ACT.Sqrt)

        def fold_1():
            nc.vector.reciprocal(out=scale_c[:], in_=std[:])
            nc.vector.tensor_sub(out=shift_c[:], in0=bias_c, in1=mean_c)

        def fold_2():
            nc.vector.tensor_mul(out=scale_c[:], in0=scale_c[:], in1=gamma_c)

        def fold_3():
            nc.vector.tensor_mul(out=shift_c[:], in0=shift_c[:], in1=scale_c[:])

        def fold_4():
            nc.vector.tensor_add(out=shift_c[:], in0=shift_c[:], in1=beta_c)

        def aggregate(g, tb, on_vector=False):
            t_cols = slice(tb * P, (tb + 1) * P)
            acc = psum.tile([P, PACK, P], F32, tag="bank")
            for j in range(PACK):
                d_cols = slice((g * PACK + j) * P, (g * PACK + j + 1) * P)
                nc.tensor.matmul_mx(
                    out=acc[:, j, :],
                    lhsT=h_codes[:, d_cols].bitcast(FP8X4),
                    lhsT_scale=h_scales[:, d_cols],
                    rhs=a_codes[:, t_cols].bitcast(FP8X4),
                    rhs_scale=a_scales[:, t_cols],
                    start=True,
                    stop=True,
                )
            src = acc[:].rearrange("p j t -> p t j")
            if on_vector:
                nc.vector.tensor_copy(out=agg_grouped[:, g, tb, :, :], in_=src)
            else:
                nc.scalar.copy(out=agg_grouped[:, g, tb, :, :], in_=src)

        def quantise_agg(g, tb0, n=PAIR):
            cols = slice(tb0 * P, (tb0 + n) * P)
            nc.vector.quantize_mx(
                out=agg_codes[:, g, cols].bitcast(FP8X4),
                scales=agg_scales[:, g, cols],
                in_=agg_grouped[:, g, tb0 : tb0 + n, :, :].rearrange("p tb t j -> p (tb t j)"),
            )

        def warm_up(passes):
            wide = w_grouped[:, 1, 0, :, :].rearrange("p m j -> p (m j)")
            unread = psum.tile([P, HALF], F32, tag="bank")
            for step in range(passes):
                nc.tensor.matmul(unread[:], lhsT=wide[:, 0:P], rhs=wide, start=True, stop=True)

        def linear_bn_relu(tb0, n, hb0, hb1):
            t_cols = slice(tb0 * P, (tb0 + n) * P)
            for hb in range(hb0, hb1):
                m_cols = slice(hb * P, (hb + 1) * P)
                acc = psum.tile([P, n * P], F32, tag="bank")
                for g in range(G):
                    nc.tensor.matmul_mx(
                        out=acc[:],
                        lhsT=w_codes[:, g, m_cols].bitcast(FP8X4),
                        lhsT_scale=w_scales[:, g, m_cols],
                        rhs=agg_codes[:, g, t_cols].bitcast(FP8X4),
                        rhs_scale=agg_scales[:, g, t_cols],
                        start=(g == 0),
                        stop=(g == G - 1),
                    )
                if (tb0, hb // HQ) in V_UNITS:
                    unit = V_UNITS.index((tb0, hb // HQ))
                    dst = y_t[:, unit : unit + n // PAIR, :, hb % HQ, :]
                    src = acc[:].rearrange("p (u j a) -> p u j a", j=PAIR * JB, a=BLK)
                else:
                    dst = y_p[:, hb, t_cols]
                    src = acc[:]
                nc.scalar.activation(
                    out=dst,
                    in_=src,
                    func=ACT.Relu,
                    bias=shift_c[:, hb : hb + 1],
                    scale=scale_c[:, hb : hb + 1],
                )

        def turn_back_vector(tb0, half):
            unit = V_UNITS.index((tb0, half))
            nc.vector.transpose(
                y_v[:, unit].rearrange("p j hb b -> p (j hb b)"),
                y_t[:, unit].rearrange("p j hb a -> p (j hb a)"),
            )

        def store_vector(tb0, half):
            unit = V_UNITS.index((tb0, half))
            rows = out[tb0 * P : (tb0 + PAIR) * P, :].rearrange("(j a) (i x c) -> i x a j c", a=BLK, i=QUADS, x=2)
            for i in (0, 2, 1, 3):
                nc.sync.dma_start(
                    out=rows[i, half],
                    in_=y_v[i * BLK : (i + 1) * BLK, unit].rearrange("p j hb b -> p j (hb b)"),
                )

        def turn_back_tensor(tb, half, on_scalar=False):
            turned = psum.tile([P, HQ, P], F32, tag="bank")
            for q in range(HQ):
                nc.tensor.transpose(turned[:, q, :], y_p[:, half * HQ + q, tb * P : (tb + 1) * P], ident_f32[:])
            dst = y_o[:, tb, :, half * HQ : (half + 1) * HQ, :].rearrange("p i q b -> p q i b")
            src = turned[:].rearrange("p q (i b) -> p q i b", b=BLK)
            if on_scalar:
                nc.scalar.copy(out=dst, in_=src)
            else:
                nc.vector.tensor_copy(out=dst, in_=src)

        def store_tensor(tb):
            nc.sync.dma_start(
                out=out_second[:, tb - CHUNK_TB, :], in_=y_o[:, tb, :, :, :].rearrange("p i hb b -> p (i hb b)")
            )

        with tc.manual_schedule():
            load_everything()
            constants()
            row_sum_vector(0)
            row_sum_scalar(1)
            turn_vectors()
            fold_0()
            row_sum_vector(2)
            row_sum_scalar(3)
            clamp(0, 2)
            fold_1()
            invert(0, 2)
            fold_2()
            normalise(0)
            normalise(1)
            transpose_a(0)
            clamp(2, 4)
            fold_3()
            invert(2, 4)
            fold_4()
            normalise(2)
            normalise(3)
            transpose_a(2)
            for tb in range(4, TB):
                row_sum_scalar(tb)
            regroup_h(0)
            quantise_a(0)
            regroup_h(1)
            quantise_h(0)
            quantise_a(2)
            for tb in range(4):
                aggregate(0, tb)
            quantise_h(1)
            for tb in range(2):
                aggregate(1, tb)
            for tb in range(2, 4):
                aggregate(1, tb)
            regroup_w(0, 0, 1)
            clamp(4, 8)
            regroup_w(0, 1, 3)
            invert(4, 8)
            regroup_w(0, 3, 4)
            for tb in range(4, TB):
                normalise(tb)
            transpose_a(4)
            transpose_a(6)
            regroup_w(0, 7, 8, nc.scalar.copy)
            quantise_w(0, 0)
            regroup_w(1, 0, 4)
            warm_up(4)
            quantise_agg(0, 0, 4)
            quantise_w(1, 0)
            quantise_agg(1, 0, 4)
            linear_bn_relu(0, 4, 0, 4)
            quantise_a(4)
            quantise_a(6)
            regroup_w(0, 4, 7)
            regroup_w(1, 4, 8)
            for tb in (4, 5):
                for g in range(G):
                    aggregate(g, tb)
            quantise_w(0, 1)
            quantise_w(1, 1)
            turn_back_vector(0, 0)
            store_vector(0, 0)
            linear_bn_relu(0, 4, 4, 8)
            turn_back_vector(2, 0)
            store_vector(2, 0)
            for g in range(G):
                quantise_agg(g, 4)
            aggregate(0, 7, True)
            aggregate(1, 7, True)
            for g in range(G):
                aggregate(g, 6)
            turn_back_vector(0, 1)
            store_vector(0, 1)
            linear_bn_relu(4, 2, 0, 8)
            for g in range(G):
                quantise_agg(g, 6)
            turn_back_vector(2, 1)
            store_vector(2, 1)
            linear_bn_relu(6, 2, 0, 4)
            turn_back_tensor(4, 0)
            turn_back_tensor(4, 1, True)
            store_tensor(4)
            turn_back_tensor(5, 0)
            turn_back_tensor(5, 1)
            store_tensor(5)
            linear_bn_relu(6, 2, 4, 8)
            turn_back_tensor(6, 0)
            turn_back_tensor(6, 1, True)
            store_tensor(6)
            turn_back_tensor(7, 0)
            turn_back_tensor(7, 1, True)
            store_tensor(7)
